import numpy as np
import ml_dtypes


def mxq(x, axis, fmt="e4m3"):
    dtype, down = {"e4m3": (ml_dtypes.float8_e4m3fn, 7), "e5m2": (ml_dtypes.float8_e5m2, 14)}[fmt]
    v = np.moveaxis(np.asarray(x, np.float32).astype(ml_dtypes.bfloat16).astype(np.float64), axis, -1)
    blocks = v.reshape(v.shape[:-1] + (-1, 32))
    amax = np.abs(blocks).max(-1, keepdims=True)
    byte = np.maximum(np.where(amax > 0, np.frexp(amax)[1] - 1 + 127, 0) - down, 1)
    scale = np.exp2(byte - 127.0)
    codes = (blocks / scale).astype(np.float32).astype(dtype).astype(np.float64)
    return np.moveaxis((codes * scale).reshape(v.shape), -1, axis)


WIDE = False


def mx_kscale(k):
    if not WIDE:
        return np.ones(k)
    levels = np.array([10, -10, 5, -5, 0])
    a = np.random.permutation(np.resize(levels, k // 512 * 4)).reshape(k // 512, 4)
    idx = np.arange(k)
    return np.exp2(a[idx // 512, idx % 128 // 32])


BF16 = ml_dtypes.bfloat16


def bf(x):
    return np.asarray(x, np.float32).astype(BF16)


def f64(x):
    return np.asarray(x).astype(np.float64)


B, S, E, H, D, XL, TOPK = 2, 256, 1024, 8, 128, 512, 8
HD = H * D
J = S * TOPK


def sigmoid(v):
    return 1.0 / (1.0 + np.exp(-v))


def setup_inputs():
    n = np.random.standard_normal
    t = mx_kscale(HD)
    k_ext = n((B, S, TOPK, HD)) * 1.5 * np.sqrt(HD)
    v_ext = (1.0 + 1.5 * n((B, S, TOPK, HD))) * t
    return {"q": bf(n((B, H, S, D)) / np.sqrt(HD)),
            "qkv": bf((0.25 + 0.5 * np.abs(n((B, H, S, D)))) * t.reshape(H, 1, D)),
            "kv_external": bf(np.stack([k_ext, v_ext], axis=-2)),
            "gate": bf(n((H, 1, 1))),
            "Wo": bf(n((E, HD)) / np.sqrt(HD) / t),
            "bo": bf(n(E) * 0.1)}


def reference(q, qkv, kv_external, gate, Wo, bo):
    kv = f64(kv_external)
    k_ext = kv[..., 0, :].reshape(B, S, TOPK, H, D).transpose(0, 3, 1, 2, 4).reshape(B, H, J, D)
    v_ext = kv[..., 1, :].reshape(B, S, TOPK, H, D).transpose(0, 3, 1, 2, 4).reshape(B, H, J, D)
    s = f64(q) @ k_ext.transpose(0, 1, 3, 2) * D ** -0.5
    e = np.exp(s - s.max(-1, keepdims=True))
    qkv_ext = (mxq(e, 3, "e4m3") @ mxq(v_ext, 2, "e4m3")) / e.sum(-1, keepdims=True)
    g = sigmoid(f64(gate))
    fused = f64(qkv) * g + qkv_ext * (1.0 - g)
    merged = fused.transpose(0, 2, 1, 3).reshape(B, S, HD)
    return (mxq(merged, 2, "e4m3") @ mxq(f64(Wo), 1, "e4m3").T) + f64(bo)

@@ -1,0 +1,288 @@
+from contextlib import ExitStack
+
+import concourse.masks as masks
+import concourse.mybir as mybir
+
+BF16 = mybir.dt.bfloat16
+F32 = mybir.dt.float32
+U32 = mybir.dt.uint32
+U8 = mybir.dt.uint8
+FP8X4 = mybir.dt.float8_e4m3fn_x4
+ACT = mybir.ActivationFunctionType
+ALU = mybir.AluOpType
+AXIS = mybir.AxisListType
+
+B, H, S, D, TOPK, E = 2, 8, 256, 128, 8, 1024
+HD = H * D
+J = S * TOPK
+P = 128
+PACK = 4
+K_PASS = P * PACK
+KEY_PASSES = J // K_PASS
+HD_PASSES = HD // K_PASS
+Q_TILES = S // P
+BANK_BLOCKS = 8
+N_OUT = 512
+PAIR = 2
+SCALE = D**-0.5
+
+FLOPS = 2 * (2 * B * H * S * J * D) + 2 * B * S * HD * E
+
+
+def tile_knnxlmultiheadsattention_pb_kernel(tc, q, qkv, kv_external, gate, Wo, bo, out):
+    nc = tc.nc
+
+    memories = kv_external.rearrange("b s t c e -> b (s t) c e").rearrange(
+        "b (g p x) c e -> b g p x c e", g=KEY_PASSES, p=P
+    )
+    q_rows = q.rearrange("b h (t p) d -> b p (h t) d", p=P)
+    qkv_rows = qkv.rearrange("b h (t p) d -> b p (h t) d", p=P)
+
+    with ExitStack() as ctx:
+        keep = ctx.enter_context(tc.tile_pool(name="keep", bufs=1))
+        raw = ctx.enter_context(tc.tile_pool(name="raw", bufs=3))
+        per_head = ctx.enter_context(tc.tile_pool(name="per_head", bufs=2))
+        per_unit = ctx.enter_context(tc.tile_pool(name="per_unit", bufs=2))
+        columns = ctx.enter_context(tc.tile_pool(name="columns", bufs=4))
+        psum_scores = ctx.enter_context(tc.psum_pool(name="psum_scores", bufs=KEY_PASSES))
+        psum_flip = ctx.enter_context(tc.psum_pool(name="psum_flip", bufs=3))
+        psum_mx = ctx.enter_context(tc.psum_pool(name="psum_mx", bufs=1))
+
+        ident = keep.tile([P, P], BF16)
+        masks.make_identity(nc, ident[:])
+
+        def flip(blocks):
+            bank = psum_flip.tile([P, BANK_BLOCKS, P], BF16)
+            for n, block in enumerate(blocks):
+                nc.tensor.transpose(bank[:, n, :], block, ident[:])
+            return bank
+
+        def words_side_by_side(bank):
+            return bank[:].rearrange("p (c x) r -> p c r x", x=PACK)
+
+        gate_rows = keep.tile([P, H], BF16)
+        nc.sync.dma_start(out=gate_rows[:], in_=gate.rearrange("h a b -> (h a b)").partition_broadcast(P))
+        q_raw = keep.tile([P, B, H * Q_TILES, D], BF16)
+        qkv_raw = keep.tile([P, B, H * Q_TILES, D], BF16)
+        wo_raw = keep.tile([P, E // P, HD], BF16)
+        bias_rows = keep.tile([P, E], BF16)
+
+        pair_tiles = {}
+
+        def load_pair(n):
+            b, first = n // (H // PAIR), (n % (H // PAIR)) * PAIR
+            cols = slice(first * D, (first + PAIR) * D)
+            k_raw = raw.tile([P, KEY_PASSES, PACK, PAIR * D], BF16)
+            v_raw = raw.tile([P, KEY_PASSES, PACK, PAIR * D], BF16)
+            for g in range(KEY_PASSES):
+                nc.sync.dma_start(out=k_raw[:, g], in_=memories[b, g, :, :, 0, cols])
+            for g in range(KEY_PASSES):
+                nc.sync.dma_start(out=v_raw[:, g], in_=memories[b, g, :, :, 1, cols])
+            pair_tiles[n] = (k_raw, v_raw)
+
+        nc.sync.dma_start(out=q_raw[:, 0], in_=q_rows[0])
+        load_pair(0)
+        nc.sync.dma_start(out=qkv_raw[:, 0], in_=qkv_rows[0])
+        load_pair(1)
+        nc.sync.dma_start(out=wo_raw[:], in_=Wo.rearrange("(a p) k -> p a k", p=P))
+        load_pair(2)
+        nc.sync.dma_start(out=q_raw[:, 1], in_=q_rows[1])
+        nc.sync.dma_start(out=qkv_raw[:, 1], in_=qkv_rows[1])
+        nc.sync.dma_start(out=bias_rows[:], in_=bo.partition_broadcast(P))
+
+        g_local = keep.tile([P, H], F32)
+        g_retrieved = keep.tile([P, H], F32)
+        nc.scalar.activation(out=g_local[:], in_=gate_rows[:], func=ACT.Sigmoid)
+        nc.scalar.activation(out=g_retrieved[:], in_=gate_rows[:], func=ACT.Sigmoid, scale=-1.0)
+
+        q_t = keep.tile([P, B, H * Q_TILES, P], BF16)
+        local_part = keep.tile([P, B, H * Q_TILES, D], F32)
+        merged = [
+            [keep.tile([P, HD], BF16, name="merged_%d_%d" % (b, t)) for t in range(Q_TILES)] for b in range(B)
+        ]
+        wo_grouped = keep.tile([P, HD_PASSES, E, PACK], BF16, align_bytes=64)
+        wo_codes = keep.tile([P, HD_PASSES, E], U32, align_bytes=64)
+        wo_scales = keep.tile([P, HD_PASSES, E], U8, align_bytes=64)
+
+        def flip_queries(b):
+            for first in range(0, H * Q_TILES, BANK_BLOCKS):
+                bank = flip([q_raw[:, b, first + n, :] for n in range(BANK_BLOCKS)])
+                nc.vector.tensor_copy(out=q_t[:, b, first : first + BANK_BLOCKS, :], in_=bank[:])
+
+        def prepare_head(b, h):
+            if h == 0:
+                flip_queries(b)
+            k_raw, v_raw = pair_tiles[(b * H + h) // PAIR]
+            cols = slice((h % PAIR) * D, (h % PAIR + 1) * D)
+
+            k_t = per_head.tile([P, KEY_PASSES * PACK, P], BF16)
+            for first in range(0, KEY_PASSES * PACK, BANK_BLOCKS):
+                bank = flip([k_raw[:, (first + n) // PACK, (first + n) % PACK, cols] for n in range(BANK_BLOCKS)])
+                nc.vector.tensor_copy(out=k_t[:, first : first + BANK_BLOCKS, :], in_=bank[:])
+
+            v_grouped = per_head.tile([P, KEY_PASSES, D, PACK], BF16, align_bytes=64)
+            nc.gpsimd.tensor_scalar(
+                out=v_grouped[:],
+                in0=v_raw[:, :, :, cols].rearrange("p g x d -> p g d x"),
+                scalar1=1.0,
+                scalar2=0.0,
+                op0=ALU.mult,
+                op1=ALU.add,
+            )
+            v_codes = per_head.tile([P, KEY_PASSES * D], U32, align_bytes=64)
+            v_scales = per_head.tile([P, KEY_PASSES * D], U8, align_bytes=64)
+            nc.vector.quantize_mx(
+                out=v_codes[:].bitcast(FP8X4),
+                scales=v_scales[:],
+                in_=v_grouped[:].rearrange("p g d x -> p (g d x)"),
+            )
+
+            blocks = slice(h * Q_TILES, (h + 1) * Q_TILES)
+            nc.gpsimd.tensor_scalar(
+                out=local_part[:, b, blocks, :],
+                in0=qkv_raw[:, b, blocks, :],
+                scalar1=g_local[:, h : h + 1],
+                scalar2=0.0,
+                op0=ALU.mult,
+                op1=ALU.add,
+            )
+            return k_t, v_codes, v_scales
+
+        def prepare_wo(n):
+            c, first = n // PACK, (n % PACK) * 2
+            bank = flip(
+                [
+                    wo_raw[:, first + a, (c * PACK + t) * P : (c * PACK + t + 1) * P]
+                    for a in range(2)
+                    for t in range(PACK)
+                ]
+            )
+            nc.scalar.copy(
+                out=wo_grouped[:, c, first * P : (first + 2) * P, :].rearrange("p (a e) t -> p a e t", a=2),
+                in_=words_side_by_side(bank),
+            )
+            if n % PACK == PACK - 1:
+                nc.vector.quantize_mx(
+                    out=wo_codes[:, c, :].bitcast(FP8X4),
+                    scales=wo_scales[:, c, :],
+                    in_=wo_grouped[:, c].rearrange("p e t -> p (e t)"),
+                )
+
+        def attend(b, h, t, k_t, v_codes, v_scales):
+            block = h * Q_TILES + t
+
+            scores = []
+            bank_max = columns.tile([P, KEY_PASSES], F32)
+            for g in range(KEY_PASSES):
+                s_bank = psum_scores.tile([P, K_PASS], F32)
+                nc.tensor.matmul(
+                    out=s_bank[:],
+                    lhsT=q_t[:, b, block, :],
+                    rhs=k_t[:, g * PACK : (g + 1) * PACK, :].rearrange("d x p -> d (x p)"),
+                    start=True,
+                    stop=True,
+                )
+                nc.vector.tensor_reduce(out=bank_max[:, g : g + 1], in_=s_bank[:], axis=AXIS.X, op=ALU.max)
+                scores.append(s_bank)
+            row_max = columns.tile([P, 1], F32)
+            nc.vector.tensor_reduce(out=row_max[:], in_=bank_max[:], axis=AXIS.X, op=ALU.max)
+            shift = columns.tile([P, 1], F32)
+            nc.vector.tensor_scalar_mul(out=shift[:], in0=row_max[:], scalar1=-SCALE)
+
+            e = per_unit.tile([P, J], BF16)
+            bank_sum = columns.tile([P, KEY_PASSES], F32)
+            for g in range(KEY_PASSES):
+                nc.scalar.activation(
+                    out=e[:, g * K_PASS : (g + 1) * K_PASS],
+                    in_=scores[g][:],
+                    func=ACT.Exp,
+                    bias=shift[:],
+                    scale=SCALE,
+                    accum_out=bank_sum[:, g : g + 1],
+                )
+
+            row_sum = columns.tile([P, 1], F32)
+            nc.vector.tensor_reduce(out=row_sum[:], in_=bank_sum[:], axis=AXIS.X, op=ALU.add)
+            inverse = columns.tile([P, 1], F32)
+            nc.vector.reciprocal(out=inverse[:], in_=row_sum[:])
+            weight = columns.tile([P, 1], F32)
+            nc.vector.tensor_mul(out=weight[:], in0=inverse[:], in1=g_retrieved[:, h : h + 1])
+
+            e_grouped = per_unit.tile([P, KEY_PASSES, P, PACK], BF16, align_bytes=64)
+            e_codes = per_unit.tile([P, KEY_PASSES * P], U32, align_bytes=64)
+            e_scales = per_unit.tile([P, KEY_PASSES * P], U8, align_bytes=64)
+            passes_in_bank = BANK_BLOCKS // PACK
+            for g in range(0, KEY_PASSES, passes_in_bank):
+                bank = flip([e[:, (g * PACK + n) * P : (g * PACK + n + 1) * P] for n in range(BANK_BLOCKS)])
+                nc.scalar.copy(out=e_grouped[:, g : g + passes_in_bank], in_=words_side_by_side(bank))
+                nc.vector.quantize_mx(
+                    out=e_codes[:, g * P : (g + passes_in_bank) * P].bitcast(FP8X4),
+                    scales=e_scales[:, g * P : (g + passes_in_bank) * P],
+                    in_=e_grouped[:, g : g + passes_in_bank].rearrange("p g r x -> p (g r x)"),
+                )
+
+            retrieved = psum_mx.tile([P, D], F32, tag="sums")
+            for g in range(KEY_PASSES):
+                nc.tensor.matmul_mx(
+                    out=retrieved[:],
+                    lhsT=e_codes[:, g * P : (g + 1) * P].bitcast(FP8X4),
+                    lhsT_scale=e_scales[:, g * P : (g + 1) * P],
+                    rhs=v_codes[:, g * D : (g + 1) * D].bitcast(FP8X4),
+                    rhs_scale=v_scales[:, g * D : (g + 1) * D],
+                    start=(g == 0),
+                    stop=(g == KEY_PASSES - 1),
+                )
+            nc.vector.scalar_tensor_tensor(
+                out=merged[b][t][:, h * D : (h + 1) * D],
+                in0=retrieved[:],
+                scalar=weight[:],
+                in1=local_part[:, b, block, :],
+                op0=ALU.mult,
+                op1=ALU.add,
+            )
+
+        def project(b, t):
+            bank = flip([merged[b][t][:, h * D : (h + 1) * D] for h in range(H)])
+            m_grouped = per_unit.tile([P, HD_PASSES, P, PACK], BF16, align_bytes=64)
+            nc.scalar.copy(out=m_grouped[:], in_=words_side_by_side(bank))
+            m_codes = per_unit.tile([P, HD_PASSES * P], U32, align_bytes=64)
+            m_scales = per_unit.tile([P, HD_PASSES * P], U8, align_bytes=64)
+            nc.vector.quantize_mx(
+                out=m_codes[:].bitcast(FP8X4),
+                scales=m_scales[:],
+                in_=m_grouped[:].rearrange("p c r t -> p (c r t)"),
+            )
+            for first in range(0, E, N_OUT):
+                projected = psum_mx.tile([P, N_OUT], F32, tag="sums")
+                for c in range(HD_PASSES):
+                    nc.tensor.matmul_mx(
+                        out=projected[:],
+                        lhsT=m_codes[:, c * P : (c + 1) * P].bitcast(FP8X4),
+                        lhsT_scale=m_scales[:, c * P : (c + 1) * P],
+                        rhs=wo_codes[:, c, first : first + N_OUT].bitcast(FP8X4),
+                        rhs_scale=wo_scales[:, c, first : first + N_OUT],
+                        start=(c == 0),
+                        stop=(c == HD_PASSES - 1),
+                    )
+                result = per_unit.tile([P, N_OUT], F32)
+                nc.vector.tensor_tensor(
+                    out=result[:], in0=projected[:], in1=bias_rows[:, first : first + N_OUT], op=ALU.add
+                )
+                nc.sync.dma_start(out=out[b, t * P : (t + 1) * P, first : first + N_OUT], in_=result[:])
+
+        heads = [(b, h) for b in range(B) for h in range(H)]
+        ready = prepare_head(0, 0)
+        for n, (b, h) in enumerate(heads):
+            following = None
+            if n + 1 < len(heads):
+                following = prepare_head(heads[n + 1][0], heads[n + 1][1])
+                if (n + 1) % PAIR == PAIR - 1 and (n + 1) // PAIR + 3 < len(heads) // PAIR:
+                    load_pair((n + 1) // PAIR + 3)
+            if b == 0:
+                prepare_wo(h)
+            for t in range(Q_TILES):
+                attend(b, h, t, ready[0], ready[1], ready[2])
+            ready = following
+            if h == H - 1:
+                for t in range(Q_TILES):
+                    project(b, t)

@@ -22,9 +22,13 @@ KEY_PASSES = J // K_PASS
 HD_PASSES = HD // K_PASS
 Q_TILES = S // P
 BANK_BLOCKS = 8
+PASSES_IN_BANK = BANK_BLOCKS // PACK
 N_OUT = 512
 PAIR = 2
 SCALE = D**-0.5
+UNITS = B * H * Q_TILES
+HEAD_STEPS = 2
+LEAD = 3
 
 FLOPS = 2 * (2 * B * H * S * J * D) + 2 * B * S * HD * E
 
@@ -39,6 +43,7 @@ def tile_knnxlmultiheadsattention_pb_kernel(tc, q, qkv, kv_external, gate, Wo, b
     qkv_rows = qkv.rearrange("b h (t p) d -> b p (h t) d", p=P)
 
     with ExitStack() as ctx:
+        ctx.enter_context(tc.manual_schedule())
         keep = ctx.enter_context(tc.tile_pool(name="keep", bufs=1))
         raw = ctx.enter_context(tc.tile_pool(name="raw", bufs=3))
         per_head = ctx.enter_context(tc.tile_pool(name="per_head", bufs=2))
@@ -59,6 +64,9 @@ def tile_knnxlmultiheadsattention_pb_kernel(tc, q, qkv, kv_external, gate, Wo, b
 
         def words_side_by_side(bank):
             return bank[:].rearrange("p (c x) r -> p c r x", x=PACK)
+
+        def unit_of(w):
+            return w // (H * Q_TILES), (w % (H * Q_TILES)) // Q_TILES, w % Q_TILES
 
         gate_rows = keep.tile([P, H], BF16)
         nc.sync.dma_start(out=gate_rows[:], in_=gate.rearrange("h a b -> (h a b)").partition_broadcast(P))
@@ -104,49 +112,60 @@ def tile_knnxlmultiheadsattention_pb_kernel(tc, q, qkv, kv_external, gate, Wo, b
         wo_codes = keep.tile([P, HD_PASSES, E], U32, align_bytes=64)
         wo_scales = keep.tile([P, HD_PASSES, E], U8, align_bytes=64)
 
-        def flip_queries(b):
-            for first in range(0, H * Q_TILES, BANK_BLOCKS):
-                bank = flip([q_raw[:, b, first + n, :] for n in range(BANK_BLOCKS)])
-                nc.vector.tensor_copy(out=q_t[:, b, first : first + BANK_BLOCKS, :], in_=bank[:])
+        key_tiles = {}
+        value_tiles = {}
 
-        def prepare_head(b, h):
-            if h == 0:
-                flip_queries(b)
-            k_raw, v_raw = pair_tiles[(b * H + h) // PAIR]
+        def prepare(step):
+            number, part = step // HEAD_STEPS, step % HEAD_STEPS
+            if number >= B * H:
+                return
+            b, h = number // H, number % H
+            k_raw, v_raw = pair_tiles[number // PAIR]
             cols = slice((h % PAIR) * D, (h % PAIR + 1) * D)
 
-            k_t = per_head.tile([P, KEY_PASSES * PACK, P], BF16)
-            for first in range(0, KEY_PASSES * PACK, BANK_BLOCKS):
-                bank = flip([k_raw[:, (first + n) // PACK, (first + n) % PACK, cols] for n in range(BANK_BLOCKS)])
-                nc.vector.tensor_copy(out=k_t[:, first : first + BANK_BLOCKS, :], in_=bank[:])
+            if part == 0:
+                if h == 0:
+                    for first in range(0, H * Q_TILES, BANK_BLOCKS):
+                        bank = flip([q_raw[:, b, first + n, :] for n in range(BANK_BLOCKS)])
+                        nc.vector.tensor_copy(out=q_t[:, b, first : first + BANK_BLOCKS, :], in_=bank[:])
+                k_t = per_head.tile([P, KEY_PASSES * PACK, P], BF16)
+                v_grouped = per_head.tile([P, KEY_PASSES, D, PACK], BF16, align_bytes=64)
+                key_tiles[number] = (k_t, v_grouped)
+            k_t, v_grouped = key_tiles[number]
 
-            v_grouped = per_head.tile([P, KEY_PASSES, D, PACK], BF16, align_bytes=64)
-            nc.gpsimd.tensor_scalar(
-                out=v_grouped[:],
-                in0=v_raw[:, :, :, cols].rearrange("p g x d -> p g d x"),
-                scalar1=1.0,
-                scalar2=0.0,
-                op0=ALU.mult,
-                op1=ALU.add,
-            )
-            v_codes = per_head.tile([P, KEY_PASSES * D], U32, align_bytes=64)
-            v_scales = per_head.tile([P, KEY_PASSES * D], U8, align_bytes=64)
-            nc.vector.quantize_mx(
-                out=v_codes[:].bitcast(FP8X4),
-                scales=v_scales[:],
-                in_=v_grouped[:].rearrange("p g d x -> p (g d x)"),
-            )
+            first = part * BANK_BLOCKS
+            bank = flip([k_raw[:, (first + n) // PACK, (first + n) % PACK, cols] for n in range(BANK_BLOCKS)])
+            nc.vector.tensor_copy(out=k_t[:, first : first + BANK_BLOCKS, :], in_=bank[:])
 
-            blocks = slice(h * Q_TILES, (h + 1) * Q_TILES)
-            nc.gpsimd.tensor_scalar(
-                out=local_part[:, b, blocks, :],
-                in0=qkv_raw[:, b, blocks, :],
-                scalar1=g_local[:, h : h + 1],
-                scalar2=0.0,
-                op0=ALU.mult,
-                op1=ALU.add,
-            )
-            return k_t, v_codes, v_scales
+            if part == 0:
+                nc.gpsimd.tensor_scalar(
+                    out=v_grouped[:],
+                    in0=v_raw[:, :, :, cols].rearrange("p g x d -> p g d x"),
+                    scalar1=1.0,
+                    scalar2=0.0,
+                    op0=ALU.mult,
+                    op1=ALU.add,
+                )
+                blocks = slice(h * Q_TILES, (h + 1) * Q_TILES)
+                nc.gpsimd.tensor_scalar(
+                    out=local_part[:, b, blocks, :],
+                    in0=qkv_raw[:, b, blocks, :],
+                    scalar1=g_local[:, h : h + 1],
+                    scalar2=0.0,
+                    op0=ALU.mult,
+                    op1=ALU.add,
+                )
+            else:
+                v_codes = per_head.tile([P, KEY_PASSES * D], U32, align_bytes=64)
+                v_scales = per_head.tile([P, KEY_PASSES * D], U8, align_bytes=64)
+                value_tiles[number] = (v_codes, v_scales)
+                nc.vector.quantize_mx(
+                    out=v_codes[:].bitcast(FP8X4),
+                    scales=v_scales[:],
+                    in_=v_grouped[:].rearrange("p g d x -> p (g d x)"),
+                )
+                if h % PAIR == PAIR - 1 and number // PAIR + 3 < B * H // PAIR:
+                    load_pair(number // PAIR + 3)
 
         def prepare_wo(n):
             c, first = n // PACK, (n % PACK) * 2
@@ -168,59 +187,96 @@ def tile_knnxlmultiheadsattention_pb_kernel(tc, q, qkv, kv_external, gate, Wo, b
                     in_=wo_grouped[:, c].rearrange("p e t -> p (e t)"),
                 )
 
-        def attend(b, h, t, k_t, v_codes, v_scales):
-            block = h * Q_TILES + t
+        score_banks = {}
+        maxima = {}
+        shifts = {}
+        exponentials = {}
+        flipped = {}
+        weights = {}
+        coded = {}
 
-            scores = []
-            bank_max = columns.tile([P, KEY_PASSES], F32)
-            for g in range(KEY_PASSES):
-                s_bank = psum_scores.tile([P, K_PASS], F32)
-                nc.tensor.matmul(
-                    out=s_bank[:],
-                    lhsT=q_t[:, b, block, :],
-                    rhs=k_t[:, g * PACK : (g + 1) * PACK, :].rearrange("d x p -> d (x p)"),
-                    start=True,
-                    stop=True,
-                )
-                nc.vector.tensor_reduce(out=bank_max[:, g : g + 1], in_=s_bank[:], axis=AXIS.X, op=ALU.max)
-                scores.append(s_bank)
+        def score_bank(w, g):
+            b, h, t = unit_of(w)
+            k_t = key_tiles[b * H + h][0]
+            if g == 0:
+                bank_max = columns.tile([P, KEY_PASSES], F32)
+                maxima[w] = bank_max
+            s_bank = psum_scores.tile([P, K_PASS], F32)
+            nc.tensor.matmul(
+                out=s_bank[:],
+                lhsT=q_t[:, b, h * Q_TILES + t, :],
+                rhs=k_t[:, g * PACK : (g + 1) * PACK, :].rearrange("d x p -> d (x p)"),
+                start=True,
+                stop=True,
+            )
+            nc.vector.tensor_reduce(out=maxima[w][:, g : g + 1], in_=s_bank[:], axis=AXIS.X, op=ALU.max)
+            score_banks[(w, g)] = s_bank
+
+        def finish_maximum(w):
             row_max = columns.tile([P, 1], F32)
-            nc.vector.tensor_reduce(out=row_max[:], in_=bank_max[:], axis=AXIS.X, op=ALU.max)
+            nc.vector.tensor_reduce(out=row_max[:], in_=maxima[w][:], axis=AXIS.X, op=ALU.max)
             shift = columns.tile([P, 1], F32)
             nc.vector.tensor_scalar_mul(out=shift[:], in0=row_max[:], scalar1=-SCALE)
+            shifts[w] = shift
 
-            e = per_unit.tile([P, J], BF16)
-            bank_sum = columns.tile([P, KEY_PASSES], F32)
-            for g in range(KEY_PASSES):
-                nc.scalar.activation(
-                    out=e[:, g * K_PASS : (g + 1) * K_PASS],
-                    in_=scores[g][:],
-                    func=ACT.Exp,
-                    bias=shift[:],
-                    scale=SCALE,
-                    accum_out=bank_sum[:, g : g + 1],
+        def exponential_bank(w, g):
+            if g == 0:
+                e = per_unit.tile([P, J], BF16)
+                bank_sum = columns.tile([P, KEY_PASSES], F32)
+                exponentials[w] = (e, bank_sum)
+            e, bank_sum = exponentials[w]
+            nc.scalar.activation(
+                out=e[:, g * K_PASS : (g + 1) * K_PASS],
+                in_=score_banks[(w, g)][:],
+                func=ACT.Exp,
+                bias=shifts[w][:],
+                scale=SCALE,
+                accum_out=bank_sum[:, g : g + 1],
+            )
+
+        def flip_pass(w, g):
+            e = exponentials[w][0]
+            if g % PASSES_IN_BANK == 0:
+                bank = psum_flip.tile([P, BANK_BLOCKS, P], BF16)
+                flipped[(w, g // PASSES_IN_BANK)] = bank
+            bank = flipped[(w, g // PASSES_IN_BANK)]
+            for x in range(PACK):
+                nc.tensor.transpose(
+                    bank[:, (g % PASSES_IN_BANK) * PACK + x, :],
+                    e[:, (g * PACK + x) * P : (g * PACK + x + 1) * P],
+                    ident[:],
                 )
 
+        def row_weight(w):
+            h = unit_of(w)[1]
             row_sum = columns.tile([P, 1], F32)
-            nc.vector.tensor_reduce(out=row_sum[:], in_=bank_sum[:], axis=AXIS.X, op=ALU.add)
+            nc.vector.tensor_reduce(out=row_sum[:], in_=exponentials[w][1][:], axis=AXIS.X, op=ALU.add)
             inverse = columns.tile([P, 1], F32)
             nc.vector.reciprocal(out=inverse[:], in_=row_sum[:])
             weight = columns.tile([P, 1], F32)
             nc.vector.tensor_mul(out=weight[:], in0=inverse[:], in1=g_retrieved[:, h : h + 1])
+            weights[w] = weight
 
+        def quantise_exponentials(w):
             e_grouped = per_unit.tile([P, KEY_PASSES, P, PACK], BF16, align_bytes=64)
             e_codes = per_unit.tile([P, KEY_PASSES * P], U32, align_bytes=64)
             e_scales = per_unit.tile([P, KEY_PASSES * P], U8, align_bytes=64)
-            passes_in_bank = BANK_BLOCKS // PACK
-            for g in range(0, KEY_PASSES, passes_in_bank):
-                bank = flip([e[:, (g * PACK + n) * P : (g * PACK + n + 1) * P] for n in range(BANK_BLOCKS)])
-                nc.scalar.copy(out=e_grouped[:, g : g + passes_in_bank], in_=words_side_by_side(bank))
-                nc.vector.quantize_mx(
-                    out=e_codes[:, g * P : (g + passes_in_bank) * P].bitcast(FP8X4),
-                    scales=e_scales[:, g * P : (g + passes_in_bank) * P],
-                    in_=e_grouped[:, g : g + passes_in_bank].rearrange("p g r x -> p (g r x)"),
+            for g in range(0, KEY_PASSES, PASSES_IN_BANK):
+                nc.scalar.copy(
+                    out=e_grouped[:, g : g + PASSES_IN_BANK],
+                    in_=words_side_by_side(flipped[(w, g // PASSES_IN_BANK)]),
                 )
+                nc.vector.quantize_mx(
+                    out=e_codes[:, g * P : (g + PASSES_IN_BANK) * P].bitcast(FP8X4),
+                    scales=e_scales[:, g * P : (g + PASSES_IN_BANK) * P],
+                    in_=e_grouped[:, g : g + PASSES_IN_BANK].rearrange("p g r x -> p (g r x)"),
+                )
+            coded[w] = (e_codes, e_scales)
 
+        def multiply_and_fuse(w):
+            b, h, t = unit_of(w)
+            e_codes, e_scales = coded[w]
+            v_codes, v_scales = value_tiles[b * H + h]
             retrieved = psum_mx.tile([P, D], F32, tag="sums")
             for g in range(KEY_PASSES):
                 nc.tensor.matmul_mx(
@@ -235,13 +291,15 @@ def tile_knnxlmultiheadsattention_pb_kernel(tc, q, qkv, kv_external, gate, Wo, b
             nc.vector.scalar_tensor_tensor(
                 out=merged[b][t][:, h * D : (h + 1) * D],
                 in0=retrieved[:],
-                scalar=weight[:],
-                in1=local_part[:, b, block, :],
+                scalar=weights[w][:],
+                in1=local_part[:, b, h * Q_TILES + t, :],
                 op0=ALU.mult,
                 op1=ALU.add,
             )
 
-        def project(b, t):
+        merged_coded = {}
+
+        def quantise_merged(b, t):
             bank = flip([merged[b][t][:, h * D : (h + 1) * D] for h in range(H)])
             m_grouped = per_unit.tile([P, HD_PASSES, P, PACK], BF16, align_bytes=64)
             nc.scalar.copy(out=m_grouped[:], in_=words_side_by_side(bank))
@@ -252,6 +310,10 @@ def tile_knnxlmultiheadsattention_pb_kernel(tc, q, qkv, kv_external, gate, Wo, b
                 scales=m_scales[:],
                 in_=m_grouped[:].rearrange("p c r t -> p (c r t)"),
             )
+            merged_coded[(b, t)] = (m_codes, m_scales)
+
+        def project(b, t):
+            m_codes, m_scales = merged_coded[(b, t)]
             for first in range(0, E, N_OUT):
                 projected = psum_mx.tile([P, N_OUT], F32, tag="sums")
                 for c in range(HD_PASSES):
@@ -270,19 +332,34 @@ def tile_knnxlmultiheadsattention_pb_kernel(tc, q, qkv, kv_external, gate, Wo, b
                 )
                 nc.sync.dma_start(out=out[b, t * P : (t + 1) * P, first : first + N_OUT], in_=result[:])
 
-        heads = [(b, h) for b in range(B) for h in range(H)]
-        ready = prepare_head(0, 0)
-        for n, (b, h) in enumerate(heads):
-            following = None
-            if n + 1 < len(heads):
-                following = prepare_head(heads[n + 1][0], heads[n + 1][1])
-                if (n + 1) % PAIR == PAIR - 1 and (n + 1) // PAIR + 3 < len(heads) // PAIR:
-                    load_pair((n + 1) // PAIR + 3)
-            if b == 0:
-                prepare_wo(h)
-            for t in range(Q_TILES):
-                attend(b, h, t, ready[0], ready[1], ready[2])
-            ready = following
-            if h == H - 1:
-                for t in range(Q_TILES):
-                    project(b, t)
+        def is_unit(w):
+            return 0 <= w < UNITS
+
+        def closes_merged(w):
+            return is_unit(w) and unit_of(w)[1] == H - 1
+
+        for step in range(LEAD - 1):
+            prepare(step)
+        for w in range(-1, UNITS + 2):
+            for g in range(KEY_PASSES):
+                if is_unit(w):
+                    exponential_bank(w, g)
+                if is_unit(w + 1):
+                    score_bank(w + 1, g)
+                if is_unit(w):
+                    flip_pass(w, g)
+            if is_unit(w + 1):
+                finish_maximum(w + 1)
+            if is_unit(w - 1):
+                multiply_and_fuse(w - 1)
+            if closes_merged(w - 2):
+                project(unit_of(w - 2)[0], unit_of(w - 2)[2])
+            if is_unit(w):
+                row_weight(w)
+            prepare(w + LEAD)
+            if is_unit(w):
+                quantise_exponentials(w)
+            if is_unit(w) and unit_of(w)[0] == 0 and unit_of(w)[2] == 1:
+                prepare_wo(unit_of(w)[1])
+            if closes_merged(w - 1):
+                quantise_merged(unit_of(w - 1)[0], unit_of(w - 1)[2])

@@ -47,6 +47,7 @@ def tile_knnxlmultiheadsattention_pb_kernel(tc, q, qkv, kv_external, gate, Wo, b
         keep = ctx.enter_context(tc.tile_pool(name="keep", bufs=1))
         raw = ctx.enter_context(tc.tile_pool(name="raw", bufs=3))
         per_head = ctx.enter_context(tc.tile_pool(name="per_head", bufs=2))
+        values = ctx.enter_context(tc.tile_pool(name="values", bufs=3))
         per_unit = ctx.enter_context(tc.tile_pool(name="per_unit", bufs=2))
         columns = ctx.enter_context(tc.tile_pool(name="columns", bufs=4))
         psum_scores = ctx.enter_context(tc.psum_pool(name="psum_scores", bufs=KEY_PASSES))
@@ -156,8 +157,8 @@ def tile_knnxlmultiheadsattention_pb_kernel(tc, q, qkv, kv_external, gate, Wo, b
                     op1=ALU.add,
                 )
             else:
-                v_codes = per_head.tile([P, KEY_PASSES * D], U32, align_bytes=64)
-                v_scales = per_head.tile([P, KEY_PASSES * D], U8, align_bytes=64)
+                v_codes = values.tile([P, KEY_PASSES * D], U32, align_bytes=64)
+                v_scales = values.tile([P, KEY_PASSES * D], U8, align_bytes=64)
                 value_tiles[number] = (v_codes, v_scales)
                 nc.vector.quantize_mx(
                     out=v_codes[:].bitcast(FP8X4),
@@ -187,90 +188,80 @@ def tile_knnxlmultiheadsattention_pb_kernel(tc, q, qkv, kv_external, gate, Wo, b
                     in_=wo_grouped[:, c].rearrange("p e t -> p (e t)"),
                 )
 
-        score_banks = {}
-        maxima = {}
-        shifts = {}
+        shifted = {}
         exponentials = {}
         flipped = {}
         weights = {}
+        grouped = {}
         coded = {}
 
-        def score_bank(w, g):
+        def scores(w):
             b, h, t = unit_of(w)
             k_t = key_tiles[b * H + h][0]
-            if g == 0:
-                bank_max = columns.tile([P, KEY_PASSES], F32)
-                maxima[w] = bank_max
-            s_bank = psum_scores.tile([P, K_PASS], F32)
-            nc.tensor.matmul(
-                out=s_bank[:],
-                lhsT=q_t[:, b, h * Q_TILES + t, :],
-                rhs=k_t[:, g * PACK : (g + 1) * PACK, :].rearrange("d x p -> d (x p)"),
-                start=True,
-                stop=True,
-            )
-            nc.vector.tensor_reduce(out=maxima[w][:, g : g + 1], in_=s_bank[:], axis=AXIS.X, op=ALU.max)
-            score_banks[(w, g)] = s_bank
-
-        def finish_maximum(w):
-            row_max = columns.tile([P, 1], F32)
-            nc.vector.tensor_reduce(out=row_max[:], in_=maxima[w][:], axis=AXIS.X, op=ALU.max)
-            shift = columns.tile([P, 1], F32)
-            nc.vector.tensor_scalar_mul(out=shift[:], in0=row_max[:], scalar1=-SCALE)
-            shifts[w] = shift
-
-        def exponential_bank(w, g):
-            if g == 0:
-                e = per_unit.tile([P, J], BF16)
-                bank_sum = columns.tile([P, KEY_PASSES], F32)
-                exponentials[w] = (e, bank_sum)
-            e, bank_sum = exponentials[w]
-            nc.scalar.activation(
-                out=e[:, g * K_PASS : (g + 1) * K_PASS],
-                in_=score_banks[(w, g)][:],
-                func=ACT.Exp,
-                bias=shifts[w][:],
-                scale=SCALE,
-                accum_out=bank_sum[:, g : g + 1],
-            )
-
-        def flip_pass(w, g):
-            e = exponentials[w][0]
-            if g % PASSES_IN_BANK == 0:
-                bank = psum_flip.tile([P, BANK_BLOCKS, P], BF16)
-                flipped[(w, g // PASSES_IN_BANK)] = bank
-            bank = flipped[(w, g // PASSES_IN_BANK)]
-            for x in range(PACK):
-                nc.tensor.transpose(
-                    bank[:, (g % PASSES_IN_BANK) * PACK + x, :],
-                    e[:, (g * PACK + x) * P : (g * PACK + x + 1) * P],
-                    ident[:],
+            negated = per_unit.tile([P, J], F32)
+            bank_min = columns.tile([P, KEY_PASSES], F32)
+            for g in range(KEY_PASSES):
+                s_bank = psum_scores.tile([P, K_PASS], F32)
+                nc.tensor.matmul(
+                    out=s_bank[:],
+                    lhsT=q_t[:, b, h * Q_TILES + t, :],
+                    rhs=k_t[:, g * PACK : (g + 1) * PACK, :].rearrange("d x p -> d (x p)"),
+                    start=True,
+                    stop=True,
                 )
+                nc.vector.tensor_scalar(
+                    out=negated[:, g * K_PASS : (g + 1) * K_PASS],
+                    in0=s_bank[:],
+                    scalar1=-SCALE,
+                    scalar2=None,
+                    op0=ALU.mult,
+                    op1=ALU.min,
+                    accum_out=bank_min[:, g : g + 1],
+                )
+            shift = columns.tile([P, 1], F32)
+            nc.vector.tensor_reduce(out=shift[:], in_=bank_min[:], axis=AXIS.X, op=ALU.min)
+            shifted[w] = (negated, shift)
+
+        def exponential(w):
+            negated, shift = shifted[w]
+            e = per_unit.tile([P, J], BF16)
+            row_sum = columns.tile([P, 1], F32)
+            nc.scalar.activation(
+                out=e[:], in_=negated[:], func=ACT.Exp, bias=shift[:], scale=-1.0, accum_out=row_sum[:]
+            )
+            exponentials[w] = (e, row_sum)
 
         def row_weight(w):
             h = unit_of(w)[1]
-            row_sum = columns.tile([P, 1], F32)
-            nc.vector.tensor_reduce(out=row_sum[:], in_=exponentials[w][1][:], axis=AXIS.X, op=ALU.add)
             inverse = columns.tile([P, 1], F32)
-            nc.vector.reciprocal(out=inverse[:], in_=row_sum[:])
+            nc.vector.reciprocal(out=inverse[:], in_=exponentials[w][1][:])
             weight = columns.tile([P, 1], F32)
             nc.vector.tensor_mul(out=weight[:], in0=inverse[:], in1=g_retrieved[:, h : h + 1])
             weights[w] = weight
 
-        def quantise_exponentials(w):
+        def flip_exponentials(w):
+            e = exponentials[w][0]
+            flipped[w] = [
+                flip([e[:, (first + n) * P : (first + n + 1) * P] for n in range(BANK_BLOCKS)])
+                for first in range(0, KEY_PASSES * PACK, BANK_BLOCKS)
+            ]
+
+        def group_exponentials(w):
             e_grouped = per_unit.tile([P, KEY_PASSES, P, PACK], BF16, align_bytes=64)
+            for n, bank in enumerate(flipped[w]):
+                nc.scalar.copy(
+                    out=e_grouped[:, n * PASSES_IN_BANK : (n + 1) * PASSES_IN_BANK], in_=words_side_by_side(bank)
+                )
+            grouped[w] = e_grouped
+
+        def quantise_exponentials(w):
             e_codes = per_unit.tile([P, KEY_PASSES * P], U32, align_bytes=64)
             e_scales = per_unit.tile([P, KEY_PASSES * P], U8, align_bytes=64)
-            for g in range(0, KEY_PASSES, PASSES_IN_BANK):
-                nc.scalar.copy(
-                    out=e_grouped[:, g : g + PASSES_IN_BANK],
-                    in_=words_side_by_side(flipped[(w, g // PASSES_IN_BANK)]),
-                )
-                nc.vector.quantize_mx(
-                    out=e_codes[:, g * P : (g + PASSES_IN_BANK) * P].bitcast(FP8X4),
-                    scales=e_scales[:, g * P : (g + PASSES_IN_BANK) * P],
-                    in_=e_grouped[:, g : g + PASSES_IN_BANK].rearrange("p g r x -> p (g r x)"),
-                )
+            nc.vector.quantize_mx(
+                out=e_codes[:].bitcast(FP8X4),
+                scales=e_scales[:],
+                in_=grouped[w][:].rearrange("p g r x -> p (g r x)"),
+            )
             coded[w] = (e_codes, e_scales)
 
         def multiply_and_fuse(w):
@@ -297,12 +288,16 @@ def tile_knnxlmultiheadsattention_pb_kernel(tc, q, qkv, kv_external, gate, Wo, b
                 op1=ALU.add,
             )
 
-        merged_coded = {}
+        merged_grouped = {}
 
-        def quantise_merged(b, t):
+        def group_merged(b, t):
             bank = flip([merged[b][t][:, h * D : (h + 1) * D] for h in range(H)])
             m_grouped = per_unit.tile([P, HD_PASSES, P, PACK], BF16, align_bytes=64)
             nc.scalar.copy(out=m_grouped[:], in_=words_side_by_side(bank))
+            merged_grouped[(b, t)] = m_grouped
+
+        def project(b, t):
+            m_grouped = merged_grouped[(b, t)]
             m_codes = per_unit.tile([P, HD_PASSES * P], U32, align_bytes=64)
             m_scales = per_unit.tile([P, HD_PASSES * P], U8, align_bytes=64)
             nc.vector.quantize_mx(
@@ -310,10 +305,6 @@ def tile_knnxlmultiheadsattention_pb_kernel(tc, q, qkv, kv_external, gate, Wo, b
                 scales=m_scales[:],
                 in_=m_grouped[:].rearrange("p c r t -> p (c r t)"),
             )
-            merged_coded[(b, t)] = (m_codes, m_scales)
-
-        def project(b, t):
-            m_codes, m_scales = merged_coded[(b, t)]
             for first in range(0, E, N_OUT):
                 projected = psum_mx.tile([P, N_OUT], F32, tag="sums")
                 for c in range(HD_PASSES):
@@ -340,26 +331,25 @@ def tile_knnxlmultiheadsattention_pb_kernel(tc, q, qkv, kv_external, gate, Wo, b
 
         for step in range(LEAD - 1):
             prepare(step)
-        for w in range(-1, UNITS + 2):
-            for g in range(KEY_PASSES):
-                if is_unit(w):
-                    exponential_bank(w, g)
-                if is_unit(w + 1):
-                    score_bank(w + 1, g)
-                if is_unit(w):
-                    flip_pass(w, g)
-            if is_unit(w + 1):
-                finish_maximum(w + 1)
-            if is_unit(w - 1):
-                multiply_and_fuse(w - 1)
-            if closes_merged(w - 2):
-                project(unit_of(w - 2)[0], unit_of(w - 2)[2])
-            if is_unit(w):
-                row_weight(w)
-            prepare(w + LEAD)
-            if is_unit(w):
-                quantise_exponentials(w)
-            if is_unit(w) and unit_of(w)[0] == 0 and unit_of(w)[2] == 1:
-                prepare_wo(unit_of(w)[1])
-            if closes_merged(w - 1):
-                quantise_merged(unit_of(w - 1)[0], unit_of(w - 1)[2])
+        for r in range(-1, UNITS + 4):
+            if is_unit(r - 2):
+                quantise_exponentials(r - 2)
+            if is_unit(r + 1):
+                scores(r + 1)
+            if is_unit(r):
+                exponential(r)
+            if is_unit(r - 1):
+                flip_exponentials(r - 1)
+            if is_unit(r - 2):
+                multiply_and_fuse(r - 2)
+            if closes_merged(r - 3):
+                project(unit_of(r - 3)[0], unit_of(r - 3)[2])
+            if is_unit(r - 1):
+                row_weight(r - 1)
+            prepare(r + LEAD)
+            if is_unit(r - 1):
+                group_exponentials(r - 1)
+            if is_unit(r) and unit_of(r)[0] == 0 and unit_of(r)[2] == 1:
+                prepare_wo(unit_of(r)[1])
+            if closes_merged(r - 2):
+                group_merged(unit_of(r - 2)[0], unit_of(r - 2)[2])

@@ -136,7 +136,7 @@ def tile_knnxlmultiheadsattention_pb_kernel(tc, q, qkv, kv_external, gate, Wo, b
 
             first = part * BANK_BLOCKS
             bank = flip([k_raw[:, (first + n) // PACK, (first + n) % PACK, cols] for n in range(BANK_BLOCKS)])
-            nc.vector.tensor_copy(out=k_t[:, first : first + BANK_BLOCKS, :], in_=bank[:])
+            nc.scalar.copy(out=k_t[:, first : first + BANK_BLOCKS, :], in_=bank[:])
 
             if part == 0:
                 nc.gpsimd.tensor_scalar(
@@ -346,9 +346,9 @@ def tile_knnxlmultiheadsattention_pb_kernel(tc, q, qkv, kv_external, gate, Wo, b
                 project(unit_of(r - 3)[0], unit_of(r - 3)[2])
             if is_unit(r - 1):
                 row_weight(r - 1)
-            prepare(r + LEAD)
             if is_unit(r - 1):
                 group_exponentials(r - 1)
+            prepare(r + LEAD)
             if is_unit(r) and unit_of(r)[0] == 0 and unit_of(r)[2] == 1:
                 prepare_wo(unit_of(r)[1])
             if closes_merged(r - 2):

@@ -28,7 +28,8 @@ PAIR = 2
 SCALE = D**-0.5
 UNITS = B * H * Q_TILES
 HEAD_STEPS = 2
-LEAD = 3
+KEY_LEAD = 3
+VALUE_LEAD = 0
 
 FLOPS = 2 * (2 * B * H * S * J * D) + 2 * B * S * HD * E
 
@@ -47,7 +48,6 @@ def tile_knnxlmultiheadsattention_pb_kernel(tc, q, qkv, kv_external, gate, Wo, b
         keep = ctx.enter_context(tc.tile_pool(name="keep", bufs=1))
         raw = ctx.enter_context(tc.tile_pool(name="raw", bufs=3))
         per_head = ctx.enter_context(tc.tile_pool(name="per_head", bufs=2))
-        values = ctx.enter_context(tc.tile_pool(name="values", bufs=3))
         per_unit = ctx.enter_context(tc.tile_pool(name="per_unit", bufs=2))
         columns = ctx.enter_context(tc.tile_pool(name="columns", bufs=4))
         psum_scores = ctx.enter_context(tc.psum_pool(name="psum_scores", bufs=KEY_PASSES))
@@ -116,57 +116,55 @@ def tile_knnxlmultiheadsattention_pb_kernel(tc, q, qkv, kv_external, gate, Wo, b
         key_tiles = {}
         value_tiles = {}
 
-        def prepare(step):
+        def prepare_keys(step):
             number, part = step // HEAD_STEPS, step % HEAD_STEPS
-            if number >= B * H:
+            if not 0 <= number < B * H:
                 return
             b, h = number // H, number % H
-            k_raw, v_raw = pair_tiles[number // PAIR]
+            k_raw = pair_tiles[number // PAIR][0]
             cols = slice((h % PAIR) * D, (h % PAIR + 1) * D)
-
             if part == 0:
                 if h == 0:
                     for first in range(0, H * Q_TILES, BANK_BLOCKS):
                         bank = flip([q_raw[:, b, first + n, :] for n in range(BANK_BLOCKS)])
                         nc.vector.tensor_copy(out=q_t[:, b, first : first + BANK_BLOCKS, :], in_=bank[:])
                 k_t = per_head.tile([P, KEY_PASSES * PACK, P], BF16)
-                v_grouped = per_head.tile([P, KEY_PASSES, D, PACK], BF16, align_bytes=64)
-                key_tiles[number] = (k_t, v_grouped)
-            k_t, v_grouped = key_tiles[number]
-
+                key_tiles[number] = k_t
+            k_t = key_tiles[number]
             first = part * BANK_BLOCKS
             bank = flip([k_raw[:, (first + n) // PACK, (first + n) % PACK, cols] for n in range(BANK_BLOCKS)])
-            nc.scalar.copy(out=k_t[:, first : first + BANK_BLOCKS, :], in_=bank[:])
-
             if part == 0:
-                nc.gpsimd.tensor_scalar(
-                    out=v_grouped[:],
-                    in0=v_raw[:, :, :, cols].rearrange("p g x d -> p g d x"),
-                    scalar1=1.0,
-                    scalar2=0.0,
-                    op0=ALU.mult,
-                    op1=ALU.add,
-                )
-                blocks = slice(h * Q_TILES, (h + 1) * Q_TILES)
-                nc.gpsimd.tensor_scalar(
-                    out=local_part[:, b, blocks, :],
-                    in0=qkv_raw[:, b, blocks, :],
-                    scalar1=g_local[:, h : h + 1],
-                    scalar2=0.0,
-                    op0=ALU.mult,
-                    op1=ALU.add,
-                )
+                nc.vector.tensor_copy(out=k_t[:, first : first + BANK_BLOCKS, :], in_=bank[:])
             else:
-                v_codes = values.tile([P, KEY_PASSES * D], U32, align_bytes=64)
-                v_scales = values.tile([P, KEY_PASSES * D], U8, align_bytes=64)
-                value_tiles[number] = (v_codes, v_scales)
+                nc.scalar.copy(out=k_t[:, first : first + BANK_BLOCKS, :], in_=bank[:])
+
+        def prepare_values(step):
+            number, part = step // HEAD_STEPS, step % HEAD_STEPS
+            if not 0 <= number < B * H:
+                return
+            b, h = number // H, number % H
+            if part == 0:
+                v_raw = pair_tiles[number // PAIR][1]
+                cols = slice((h % PAIR) * D, (h % PAIR + 1) * D)
+                v_grouped = per_head.tile([P, KEY_PASSES, D, PACK], BF16, align_bytes=64)
+                nc.vector.tensor_copy(out=v_grouped[:], in_=v_raw[:, :, :, cols].rearrange("p g x d -> p g d x"))
+                value_tiles[number] = v_grouped
+                if h % PAIR == PAIR - 1 and number // PAIR + 3 < B * H // PAIR:
+                    load_pair(number // PAIR + 3)
+            else:
+                v_grouped = value_tiles[number]
+                v_codes = per_head.tile([P, KEY_PASSES * D], U32, align_bytes=64)
+                v_scales = per_head.tile([P, KEY_PASSES * D], U8, align_bytes=64)
                 nc.vector.quantize_mx(
                     out=v_codes[:].bitcast(FP8X4),
                     scales=v_scales[:],
                     in_=v_grouped[:].rearrange("p g d x -> p (g d x)"),
                 )
-                if h % PAIR == PAIR - 1 and number // PAIR + 3 < B * H // PAIR:
-                    load_pair(number // PAIR + 3)
+                value_tiles[number] = (v_codes, v_scales)
+                blocks = slice(h * Q_TILES, (h + 1) * Q_TILES)
+                nc.vector.tensor_scalar_mul(
+                    out=local_part[:, b, blocks, :], in0=qkv_raw[:, b, blocks, :], scalar1=g_local[:, h : h + 1]
+                )
 
         def prepare_wo(n):
             c, first = n // PACK, (n % PACK) * 2
@@ -197,7 +195,7 @@ def tile_knnxlmultiheadsattention_pb_kernel(tc, q, qkv, kv_external, gate, Wo, b
 
         def scores(w):
             b, h, t = unit_of(w)
-            k_t = key_tiles[b * H + h][0]
+            k_t = key_tiles[b * H + h]
             negated = per_unit.tile([P, J], F32)
             bank_min = columns.tile([P, KEY_PASSES], F32)
             for g in range(KEY_PASSES):
@@ -329,8 +327,8 @@ def tile_knnxlmultiheadsattention_pb_kernel(tc, q, qkv, kv_external, gate, Wo, b
         def closes_merged(w):
             return is_unit(w) and unit_of(w)[1] == H - 1
 
-        for step in range(LEAD - 1):
-            prepare(step)
+        for step in range(KEY_LEAD - 1):
+            prepare_keys(step)
         for r in range(-1, UNITS + 4):
             if is_unit(r - 2):
                 quantise_exponentials(r - 2)
@@ -348,8 +346,9 @@ def tile_knnxlmultiheadsattention_pb_kernel(tc, q, qkv, kv_external, gate, Wo, b
                 row_weight(r - 1)
             if is_unit(r - 1):
                 group_exponentials(r - 1)
-            prepare(r + LEAD)
-            if is_unit(r) and unit_of(r)[0] == 0 and unit_of(r)[2] == 1:
-                prepare_wo(unit_of(r)[1])
+            prepare_keys(r + KEY_LEAD)
+            prepare_values(r + VALUE_LEAD)
+            if UNITS // 4 <= r < UNITS // 2:
+                prepare_wo(r - UNITS // 4)
             if closes_merged(r - 2):
                 group_merged(unit_of(r - 2)[0], unit_of(r - 2)[2])

@@ -22,7 +22,9 @@ KEY_PASSES = J // K_PASS
 HD_PASSES = HD // K_PASS
 Q_TILES = S // P
 BANK_BLOCKS = 8
-PASSES_IN_BANK = BANK_BLOCKS // PACK
+PAIRS = 2
+BANK_WORD_BLOCKS = 4
+PASSES_IN_BANK = BANK_WORD_BLOCKS // PAIRS
 N_OUT = 512
 PAIR = 2
 SCALE = D**-0.5
@@ -56,11 +58,19 @@ def tile_knnxlmultiheadsattention_pb_kernel(tc, q, qkv, kv_external, gate, Wo, b
 
         ident = keep.tile([P, P], BF16)
         masks.make_identity(nc, ident[:])
+        ident_words = keep.tile([P, P], F32)
+        masks.make_identity(nc, ident_words[:])
 
         def flip(blocks):
-            bank = psum_flip.tile([P, BANK_BLOCKS, P], BF16)
+            bank = psum_flip.tile([P, BANK_BLOCKS, P], BF16, tag="flip")
             for n, block in enumerate(blocks):
                 nc.tensor.transpose(bank[:, n, :], block, ident[:])
+            return bank
+
+        def flip_words(blocks):
+            bank = psum_flip.tile([P, BANK_WORD_BLOCKS, P], F32, tag="flip")
+            for n, block in enumerate(blocks):
+                nc.tensor.transpose(bank[:, n, :], block, ident_words[:])
             return bank
 
         def words_side_by_side(bank):
@@ -201,9 +211,9 @@ def tile_knnxlmultiheadsattention_pb_kernel(tc, q, qkv, kv_external, gate, Wo, b
             for g in range(KEY_PASSES):
                 s_bank = psum_scores.tile([P, K_PASS], F32)
                 nc.tensor.matmul(
-                    out=s_bank[:],
+                    out=s_bank[:].rearrange("q (u p j) -> q u p j", u=PAIRS, j=2),
                     lhsT=q_t[:, b, h * Q_TILES + t, :],
-                    rhs=k_t[:, g * PACK : (g + 1) * PACK, :].rearrange("d x p -> d (x p)"),
+                    rhs=k_t[:, g * PACK : (g + 1) * PACK, :].rearrange("d (u j) p -> d u p j", u=PAIRS),
                     start=True,
                     stop=True,
                 )
@@ -238,17 +248,19 @@ def tile_knnxlmultiheadsattention_pb_kernel(tc, q, qkv, kv_external, gate, Wo, b
             weights[w] = weight
 
         def flip_exponentials(w):
-            e = exponentials[w][0]
+            words = exponentials[w][0][:].bitcast(F32)
             flipped[w] = [
-                flip([e[:, (first + n) * P : (first + n + 1) * P] for n in range(BANK_BLOCKS)])
-                for first in range(0, KEY_PASSES * PACK, BANK_BLOCKS)
+                flip_words([words[:, (first + n) * P : (first + n + 1) * P] for n in range(BANK_WORD_BLOCKS)])
+                for first in range(0, KEY_PASSES * PAIRS, BANK_WORD_BLOCKS)
             ]
 
         def group_exponentials(w):
-            e_grouped = per_unit.tile([P, KEY_PASSES, P, PACK], BF16, align_bytes=64)
+            e_grouped = per_unit.tile([P, KEY_PASSES * P * PACK], BF16, align_bytes=64)
+            words = e_grouped[:].bitcast(F32).rearrange("p (g r u) -> p g r u", g=KEY_PASSES, u=PAIRS)
             for n, bank in enumerate(flipped[w]):
                 nc.scalar.copy(
-                    out=e_grouped[:, n * PASSES_IN_BANK : (n + 1) * PASSES_IN_BANK], in_=words_side_by_side(bank)
+                    out=words[:, n * PASSES_IN_BANK : (n + 1) * PASSES_IN_BANK],
+                    in_=bank[:].rearrange("p (g u) r -> p g r u", u=PAIRS),
                 )
             grouped[w] = e_grouped
 
@@ -258,7 +270,7 @@ def tile_knnxlmultiheadsattention_pb_kernel(tc, q, qkv, kv_external, gate, Wo, b
             nc.vector.quantize_mx(
                 out=e_codes[:].bitcast(FP8X4),
                 scales=e_scales[:],
-                in_=grouped[w][:].rearrange("p g r x -> p (g r x)"),
+                in_=grouped[w][:],
             )
             coded[w] = (e_codes, e_scales)
 

@@ -22,6 +22,7 @@ KEY_PASSES = J // K_PASS
 HD_PASSES = HD // K_PASS
 Q_TILES = S // P
 BANK_BLOCKS = 8
+K_WORDS = K_PASS // 2
 PAIRS = 2
 BANK_WORD_BLOCKS = 4
 PASSES_IN_BANK = BANK_WORD_BLOCKS // PAIRS
@@ -31,7 +32,7 @@ SCALE = D**-0.5
 UNITS = B * H * Q_TILES
 HEAD_STEPS = 2
 KEY_LEAD = 3
-VALUE_LEAD = 0
+VALUE_LEAD = 1
 
 FLOPS = 2 * (2 * B * H * S * J * D) + 2 * B * S * HD * E
 
@@ -72,9 +73,6 @@ def tile_knnxlmultiheadsattention_pb_kernel(tc, q, qkv, kv_external, gate, Wo, b
             for n, block in enumerate(blocks):
                 nc.tensor.transpose(bank[:, n, :], block, ident_words[:])
             return bank
-
-        def words_side_by_side(bank):
-            return bank[:].rearrange("p (c x) r -> p c r x", x=PACK)
 
         def unit_of(w):
             return w // (H * Q_TILES), (w % (H * Q_TILES)) // Q_TILES, w % Q_TILES
@@ -119,7 +117,7 @@ def tile_knnxlmultiheadsattention_pb_kernel(tc, q, qkv, kv_external, gate, Wo, b
         merged = [
             [keep.tile([P, HD], BF16, name="merged_%d_%d" % (b, t)) for t in range(Q_TILES)] for b in range(B)
         ]
-        wo_grouped = keep.tile([P, HD_PASSES, E, PACK], BF16, align_bytes=64)
+        wo_grouped = keep.tile([P, HD_PASSES, E * PACK], BF16, align_bytes=64)
         wo_codes = keep.tile([P, HD_PASSES, E], U32, align_bytes=64)
         wo_scales = keep.tile([P, HD_PASSES, E], U8, align_bytes=64)
 
@@ -143,10 +141,7 @@ def tile_knnxlmultiheadsattention_pb_kernel(tc, q, qkv, kv_external, gate, Wo, b
             k_t = key_tiles[number]
             first = part * BANK_BLOCKS
             bank = flip([k_raw[:, (first + n) // PACK, (first + n) % PACK, cols] for n in range(BANK_BLOCKS)])
-            if part == 0:
-                nc.vector.tensor_copy(out=k_t[:, first : first + BANK_BLOCKS, :], in_=bank[:])
-            else:
-                nc.scalar.copy(out=k_t[:, first : first + BANK_BLOCKS, :], in_=bank[:])
+            nc.scalar.copy(out=k_t[:, first : first + BANK_BLOCKS, :], in_=bank[:])
 
         def prepare_values(step):
             number, part = step // HEAD_STEPS, step % HEAD_STEPS
@@ -157,7 +152,15 @@ def tile_knnxlmultiheadsattention_pb_kernel(tc, q, qkv, kv_external, gate, Wo, b
                 v_raw = pair_tiles[number // PAIR][1]
                 cols = slice((h % PAIR) * D, (h % PAIR + 1) * D)
                 v_grouped = per_head.tile([P, KEY_PASSES, D, PACK], BF16, align_bytes=64)
-                nc.vector.tensor_copy(out=v_grouped[:], in_=v_raw[:, :, :, cols].rearrange("p g x d -> p g d x"))
+                for g in range(KEY_PASSES):
+                    nc.gpsimd.tensor_scalar(
+                        out=v_grouped[:, g],
+                        in0=v_raw[:, g, :, cols].rearrange("p x d -> p d x"),
+                        scalar1=1.0,
+                        scalar2=0.0,
+                        op0=ALU.mult,
+                        op1=ALU.add,
+                    )
                 value_tiles[number] = v_grouped
                 if h % PAIR == PAIR - 1 and number // PAIR + 3 < B * H // PAIR:
                     load_pair(number // PAIR + 3)
@@ -178,22 +181,21 @@ def tile_knnxlmultiheadsattention_pb_kernel(tc, q, qkv, kv_external, gate, Wo, b
 
         def prepare_wo(n):
             c, first = n // PACK, (n % PACK) * 2
-            bank = flip(
-                [
-                    wo_raw[:, first + a, (c * PACK + t) * P : (c * PACK + t + 1) * P]
-                    for a in range(2)
-                    for t in range(PACK)
-                ]
+            words = wo_raw[:].bitcast(F32)
+            bank = flip_words(
+                [words[:, first + a, c * K_WORDS + u : (c + 1) * K_WORDS : PAIRS] for a in range(2) for u in range(PAIRS)]
             )
             nc.scalar.copy(
-                out=wo_grouped[:, c, first * P : (first + 2) * P, :].rearrange("p (a e) t -> p a e t", a=2),
-                in_=words_side_by_side(bank),
+                out=wo_grouped[:, c, first * P * PACK : (first + 2) * P * PACK]
+                .bitcast(F32)
+                .rearrange("p (a e u) -> p a e u", a=2, u=PAIRS),
+                in_=bank[:].rearrange("p (a u) e -> p a e u", u=PAIRS),
             )
             if n % PACK == PACK - 1:
                 nc.vector.quantize_mx(
                     out=wo_codes[:, c, :].bitcast(FP8X4),
                     scales=wo_scales[:, c, :],
-                    in_=wo_grouped[:, c].rearrange("p e t -> p (e t)"),
+                    in_=wo_grouped[:, c],
                 )
 
         shifted = {}
@@ -301,9 +303,15 @@ def tile_knnxlmultiheadsattention_pb_kernel(tc, q, qkv, kv_external, gate, Wo, b
         merged_grouped = {}
 
         def group_merged(b, t):
-            bank = flip([merged[b][t][:, h * D : (h + 1) * D] for h in range(H)])
-            m_grouped = per_unit.tile([P, HD_PASSES, P, PACK], BF16, align_bytes=64)
-            nc.scalar.copy(out=m_grouped[:], in_=words_side_by_side(bank))
+            words = merged[b][t][:].bitcast(F32)
+            bank = flip_words(
+                [words[:, c * K_WORDS + u : (c + 1) * K_WORDS : PAIRS] for c in range(HD_PASSES) for u in range(PAIRS)]
+            )
+            m_grouped = per_unit.tile([P, HD_PASSES * P * PACK], BF16, align_bytes=64)
+            nc.scalar.copy(
+                out=m_grouped[:].bitcast(F32).rearrange("p (c r u) -> p c r u", c=HD_PASSES, u=PAIRS),
+                in_=bank[:].rearrange("p (c u) r -> p c r u", u=PAIRS),
+            )
             merged_grouped[(b, t)] = m_grouped
 
         def project(b, t):
@@ -313,7 +321,7 @@ def tile_knnxlmultiheadsattention_pb_kernel(tc, q, qkv, kv_external, gate, Wo, b
             nc.vector.quantize_mx(
                 out=m_codes[:].bitcast(FP8X4),
                 scales=m_scales[:],
-                in_=m_grouped[:].rearrange("p c r t -> p (c r t)"),
+                in_=m_grouped[:],
             )
             for first in range(0, E, N_OUT):
                 projected = psum_mx.tile([P, N_OUT], F32, tag="sums")

@@ -43,6 +43,7 @@ def tile_knnxlmultiheadsattention_pb_kernel(tc, q, qkv, kv_external, gate, Wo, b
     memories = kv_external.rearrange("b s t c e -> b (s t) c e").rearrange(
         "b (g p x) c e -> b g p x c e", g=KEY_PASSES, p=P
     )
+    key_rows = kv_external.rearrange("b s t c e -> b (s t) c e").rearrange("b (m i u) c e -> b m i u c e", i=P, u=PAIRS)
     q_rows = q.rearrange("b h (t p) d -> b p (h t) d", p=P)
     qkv_rows = qkv.rearrange("b h (t p) d -> b p (h t) d", p=P)
 
@@ -89,10 +90,10 @@ def tile_knnxlmultiheadsattention_pb_kernel(tc, q, qkv, kv_external, gate, Wo, b
         def load_pair(n):
             b, first = n // (H // PAIR), (n % (H // PAIR)) * PAIR
             cols = slice(first * D, (first + PAIR) * D)
-            k_raw = raw.tile([P, KEY_PASSES, PACK, PAIR * D], BF16)
+            k_raw = raw.tile([P, KEY_PASSES * 2, PAIRS, PAIR * D], BF16)
             v_raw = raw.tile([P, KEY_PASSES, PACK, PAIR * D], BF16)
-            for g in range(KEY_PASSES):
-                nc.sync.dma_start(out=k_raw[:, g], in_=memories[b, g, :, :, 0, cols])
+            for m in range(KEY_PASSES * 2):
+                nc.sync.dma_start(out=k_raw[:, m], in_=key_rows[b, m, :, :, 0, cols])
             for g in range(KEY_PASSES):
                 nc.sync.dma_start(out=v_raw[:, g], in_=memories[b, g, :, :, 1, cols])
             pair_tiles[n] = (k_raw, v_raw)
@@ -140,7 +141,14 @@ def tile_knnxlmultiheadsattention_pb_kernel(tc, q, qkv, kv_external, gate, Wo, b
                 key_tiles[number] = k_t
             k_t = key_tiles[number]
             first = part * BANK_BLOCKS
-            bank = flip([k_raw[:, (first + n) // PACK, (first + n) % PACK, cols] for n in range(BANK_BLOCKS)])
+            bank = flip(
+                [
+                    k_raw[:, 2 * g + n, u, cols]
+                    for g in range(first // PACK, (first + BANK_BLOCKS) // PACK)
+                    for u in range(PAIRS)
+                    for n in range(2)
+                ]
+            )
             nc.scalar.copy(out=k_t[:, first : first + BANK_BLOCKS, :], in_=bank[:])
 
         def prepare_values(step):
@@ -154,8 +162,8 @@ def tile_knnxlmultiheadsattention_pb_kernel(tc, q, qkv, kv_external, gate, Wo, b
                 v_grouped = per_head.tile([P, KEY_PASSES, D, PACK], BF16, align_bytes=64)
                 for g in range(KEY_PASSES):
                     nc.gpsimd.tensor_scalar(
-                        out=v_grouped[:, g],
-                        in0=v_raw[:, g, :, cols].rearrange("p x d -> p d x"),
+                        out=v_grouped[:, g].rearrange("p d (u j) -> p d u j", u=PAIRS),
+                        in0=v_raw[:, g, :, cols].rearrange("p (j u) d -> p d u j", u=PAIRS),
                         scalar1=1.0,
                         scalar2=0.0,
                         op0=ALU.mult,
@@ -213,9 +221,9 @@ def tile_knnxlmultiheadsattention_pb_kernel(tc, q, qkv, kv_external, gate, Wo, b
             for g in range(KEY_PASSES):
                 s_bank = psum_scores.tile([P, K_PASS], F32)
                 nc.tensor.matmul(
-                    out=s_bank[:].rearrange("q (u p j) -> q u p j", u=PAIRS, j=2),
+                    out=s_bank[:],
                     lhsT=q_t[:, b, h * Q_TILES + t, :],
-                    rhs=k_t[:, g * PACK : (g + 1) * PACK, :].rearrange("d (u j) p -> d u p j", u=PAIRS),
+                    rhs=k_t[:, g * PACK : (g + 1) * PACK, :].rearrange("d x p -> d (x p)"),
                     start=True,
                     stop=True,
                 )

@@ -28,11 +28,14 @@ BANK_WORD_BLOCKS = 4
 PASSES_IN_BANK = BANK_WORD_BLOCKS // PAIRS
 N_OUT = 512
 PAIR = 2
+PAIR_BLOCKS = PAIR * Q_TILES
 SCALE = D**-0.5
 UNITS = B * H * Q_TILES
 HEAD_STEPS = 2
 KEY_LEAD = 3
-VALUE_LEAD = 1
+QUERY_LEAD = 3
+WO_PIECES = 8
+WO_START = 4
 
 FLOPS = 2 * (2 * B * H * S * J * D) + 2 * B * S * HD * E
 
@@ -54,6 +57,8 @@ def tile_knnxlmultiheadsattention_pb_kernel(tc, q, qkv, kv_external, gate, Wo, b
         per_head = ctx.enter_context(tc.tile_pool(name="per_head", bufs=2))
         per_unit = ctx.enter_context(tc.tile_pool(name="per_unit", bufs=2))
         columns = ctx.enter_context(tc.tile_pool(name="columns", bufs=4))
+        results = ctx.enter_context(tc.tile_pool(name="results", bufs=4))
+        merged_code_pool = ctx.enter_context(tc.tile_pool(name="merged_codes", bufs=4))
         psum_scores = ctx.enter_context(tc.psum_pool(name="psum_scores", bufs=KEY_PASSES))
         psum_flip = ctx.enter_context(tc.psum_pool(name="psum_flip", bufs=3))
         psum_mx = ctx.enter_context(tc.psum_pool(name="psum_mx", bufs=1))
@@ -79,7 +84,6 @@ def tile_knnxlmultiheadsattention_pb_kernel(tc, q, qkv, kv_external, gate, Wo, b
             return w // (H * Q_TILES), (w % (H * Q_TILES)) // Q_TILES, w % Q_TILES
 
         gate_rows = keep.tile([P, H], BF16)
-        nc.sync.dma_start(out=gate_rows[:], in_=gate.rearrange("h a b -> (h a b)").partition_broadcast(P))
         q_raw = keep.tile([P, B, H * Q_TILES, D], BF16)
         qkv_raw = keep.tile([P, B, H * Q_TILES, D], BF16)
         wo_raw = keep.tile([P, E // P, HD], BF16)
@@ -90,189 +94,232 @@ def tile_knnxlmultiheadsattention_pb_kernel(tc, q, qkv, kv_external, gate, Wo, b
         def load_pair(n):
             b, first = n // (H // PAIR), (n % (H // PAIR)) * PAIR
             cols = slice(first * D, (first + PAIR) * D)
+            blocks = slice(first * Q_TILES, (first + PAIR) * Q_TILES)
             k_raw = raw.tile([P, KEY_PASSES * 2, PAIRS, PAIR * D], BF16)
             v_raw = raw.tile([P, KEY_PASSES, PACK, PAIR * D], BF16)
+            nc.sync.dma_start(out=q_raw[:, b, blocks], in_=q_rows[b][:, blocks])
             for m in range(KEY_PASSES * 2):
                 nc.sync.dma_start(out=k_raw[:, m], in_=key_rows[b, m, :, :, 0, cols])
             for g in range(KEY_PASSES):
                 nc.sync.dma_start(out=v_raw[:, g], in_=memories[b, g, :, :, 1, cols])
+            nc.sync.dma_start(out=qkv_raw[:, b, blocks], in_=qkv_rows[b][:, blocks])
             pair_tiles[n] = (k_raw, v_raw)
 
-        nc.sync.dma_start(out=q_raw[:, 0], in_=q_rows[0])
         load_pair(0)
-        nc.sync.dma_start(out=qkv_raw[:, 0], in_=qkv_rows[0])
+        nc.sync.dma_start(out=gate_rows[:], in_=gate.rearrange("h a b -> (h a b)").partition_broadcast(P))
         load_pair(1)
         nc.sync.dma_start(out=wo_raw[:], in_=Wo.rearrange("(a p) k -> p a k", p=P))
         load_pair(2)
-        nc.sync.dma_start(out=q_raw[:, 1], in_=q_rows[1])
-        nc.sync.dma_start(out=qkv_raw[:, 1], in_=qkv_rows[1])
         nc.sync.dma_start(out=bias_rows[:], in_=bo.partition_broadcast(P))
 
         g_local = keep.tile([P, H], F32)
-        g_retrieved = keep.tile([P, H], F32)
-        nc.scalar.activation(out=g_local[:], in_=gate_rows[:], func=ACT.Sigmoid)
-        nc.scalar.activation(out=g_retrieved[:], in_=gate_rows[:], func=ACT.Sigmoid, scale=-1.0)
+        retrieved_divisor = keep.tile([P, H], F32)
+
+        def prepare_gates():
+            exp_minus = keep.tile([P, H], F32)
+            exp_plus = keep.tile([P, H], F32)
+            local_divisor = keep.tile([P, H], F32)
+            nc.scalar.activation(out=exp_minus[:], in_=gate_rows[:], func=ACT.Exp, scale=-1.0)
+            nc.scalar.activation(out=exp_plus[:], in_=gate_rows[:], func=ACT.Exp)
+            nc.vector.tensor_scalar_add(out=local_divisor[:], in0=exp_minus[:], scalar1=1.0)
+            nc.vector.tensor_scalar_add(out=retrieved_divisor[:], in0=exp_plus[:], scalar1=1.0)
+            nc.vector.reciprocal(out=g_local[:], in_=local_divisor[:])
 
         q_t = keep.tile([P, B, H * Q_TILES, P], BF16)
         local_part = keep.tile([P, B, H * Q_TILES, D], F32)
         merged = [
             [keep.tile([P, HD], BF16, name="merged_%d_%d" % (b, t)) for t in range(Q_TILES)] for b in range(B)
         ]
-        wo_grouped = keep.tile([P, HD_PASSES, E * PACK], BF16, align_bytes=64)
         wo_codes = keep.tile([P, HD_PASSES, E], U32, align_bytes=64)
         wo_scales = keep.tile([P, HD_PASSES, E], U8, align_bytes=64)
 
         key_tiles = {}
         value_tiles = {}
 
-        def prepare_keys(step):
-            number, part = step // HEAD_STEPS, step % HEAD_STEPS
-            if not 0 <= number < B * H:
-                return
-            b, h = number // H, number % H
+        def prepare_queries(n):
+            b, first = n // (H // PAIR), (n % (H // PAIR)) * PAIR_BLOCKS
+            blocks = slice(first, first + PAIR_BLOCKS)
+            bank = flip([q_raw[:, b, first + m, :] for m in range(PAIR_BLOCKS)])
+            nc.vector.tensor_copy(out=q_t[:, b, blocks, :], in_=bank[:, :PAIR_BLOCKS, :])
+
+        key_banks = {}
+
+        def flip_keys(number, passes):
+            h = number % H
             k_raw = pair_tiles[number // PAIR][0]
             cols = slice((h % PAIR) * D, (h % PAIR + 1) * D)
-            if part == 0:
-                if h == 0:
-                    for first in range(0, H * Q_TILES, BANK_BLOCKS):
-                        bank = flip([q_raw[:, b, first + n, :] for n in range(BANK_BLOCKS)])
-                        nc.vector.tensor_copy(out=q_t[:, b, first : first + BANK_BLOCKS, :], in_=bank[:])
+            key_banks[number] = flip([k_raw[:, 2 * g + n, u, cols] for g in passes for u in range(PAIRS) for n in range(2)])
+
+        def copy_keys(number, passes, copy):
+            if passes[0] == 0:
                 k_t = per_head.tile([P, KEY_PASSES * PACK, P], BF16)
                 key_tiles[number] = k_t
-            k_t = key_tiles[number]
-            first = part * BANK_BLOCKS
-            bank = flip(
-                [
-                    k_raw[:, 2 * g + n, u, cols]
-                    for g in range(first // PACK, (first + BANK_BLOCKS) // PACK)
-                    for u in range(PAIRS)
-                    for n in range(2)
-                ]
-            )
-            nc.scalar.copy(out=k_t[:, first : first + BANK_BLOCKS, :], in_=bank[:])
+            blocks = len(passes) * PACK
+            first = passes[0] * PACK
+            copy(out=key_tiles[number][:, first : first + blocks, :], in_=key_banks[number][:, :blocks, :])
 
-        def prepare_values(step):
+        def key_step(step):
             number, part = step // HEAD_STEPS, step % HEAD_STEPS
-            if not 0 <= number < B * H:
+            return (number, range(part * 2, part * 2 + 2)) if number < B * H else None
+
+        grouped_values = {}
+
+        def regroup_values(number, half):
+            if number == B * H:
                 return
-            b, h = number // H, number % H
-            if part == 0:
-                v_raw = pair_tiles[number // PAIR][1]
-                cols = slice((h % PAIR) * D, (h % PAIR + 1) * D)
-                v_grouped = per_head.tile([P, KEY_PASSES, D, PACK], BF16, align_bytes=64)
-                for g in range(KEY_PASSES):
-                    nc.gpsimd.tensor_scalar(
-                        out=v_grouped[:, g].rearrange("p d (u j) -> p d u j", u=PAIRS),
-                        in0=v_raw[:, g, :, cols].rearrange("p (j u) d -> p d u j", u=PAIRS),
-                        scalar1=1.0,
-                        scalar2=0.0,
-                        op0=ALU.mult,
-                        op1=ALU.add,
-                    )
-                value_tiles[number] = v_grouped
-                if h % PAIR == PAIR - 1 and number // PAIR + 3 < B * H // PAIR:
-                    load_pair(number // PAIR + 3)
-            else:
-                v_grouped = value_tiles[number]
+            h = number % H
+            v_raw = pair_tiles[number // PAIR][1]
+            cols = slice((h % PAIR) * D, (h % PAIR + 1) * D)
+            v_grouped = keep.tile([P, 2, D, PACK], BF16, align_bytes=64, name="v_grouped_%d" % half)
+            for n in range(2):
+                nc.gpsimd.tensor_scalar(
+                    out=v_grouped[:, n].rearrange("p d (u j) -> p d u j", u=PAIRS),
+                    in0=v_raw[:, half * 2 + n, :, cols].rearrange("p (j u) d -> p d u j", u=PAIRS),
+                    scalar1=1.0,
+                    scalar2=0.0,
+                    op0=ALU.mult,
+                    op1=ALU.add,
+                )
+            grouped_values[half] = v_grouped
+            if h % PAIR == PAIR - 1 and half == 1 and number // PAIR + 3 < B * H // PAIR:
+                load_pair(number // PAIR + 3)
+
+        def quantise_values(number, half):
+            if half == 0:
                 v_codes = per_head.tile([P, KEY_PASSES * D], U32, align_bytes=64)
                 v_scales = per_head.tile([P, KEY_PASSES * D], U8, align_bytes=64)
-                nc.vector.quantize_mx(
-                    out=v_codes[:].bitcast(FP8X4),
-                    scales=v_scales[:],
-                    in_=v_grouped[:].rearrange("p g d x -> p (g d x)"),
-                )
                 value_tiles[number] = (v_codes, v_scales)
-                blocks = slice(h * Q_TILES, (h + 1) * Q_TILES)
-                nc.vector.tensor_scalar_mul(
-                    out=local_part[:, b, blocks, :], in0=qkv_raw[:, b, blocks, :], scalar1=g_local[:, h : h + 1]
-                )
+            v_codes, v_scales = value_tiles[number]
+            cols = slice(half * 2 * D, (half * 2 + 2) * D)
+            nc.vector.quantize_mx(
+                out=v_codes[:, cols].bitcast(FP8X4),
+                scales=v_scales[:, cols],
+                in_=grouped_values[half][:].rearrange("p g d x -> p (g d x)"),
+            )
 
-        def prepare_wo(n):
+        def weigh_local(number):
+            b, h = number // H, number % H
+            blocks = slice(h * Q_TILES, (h + 1) * Q_TILES)
+            nc.gpsimd.tensor_scalar(
+                out=local_part[:, b, blocks, :],
+                in0=qkv_raw[:, b, blocks, :],
+                scalar1=g_local[:, h : h + 1],
+                scalar2=0.0,
+                op0=ALU.mult,
+                op1=ALU.add,
+            )
+
+        wo_banks = {}
+        wo_pieces = {}
+
+        def flip_wo(n):
             c, first = n // PACK, (n % PACK) * 2
             words = wo_raw[:].bitcast(F32)
-            bank = flip_words(
+            wo_banks[n] = flip_words(
                 [words[:, first + a, c * K_WORDS + u : (c + 1) * K_WORDS : PAIRS] for a in range(2) for u in range(PAIRS)]
             )
-            nc.scalar.copy(
-                out=wo_grouped[:, c, first * P * PACK : (first + 2) * P * PACK]
-                .bitcast(F32)
-                .rearrange("p (a e u) -> p a e u", a=2, u=PAIRS),
-                in_=bank[:].rearrange("p (a u) e -> p a e u", u=PAIRS),
-            )
-            if n % PACK == PACK - 1:
-                nc.vector.quantize_mx(
-                    out=wo_codes[:, c, :].bitcast(FP8X4),
-                    scales=wo_scales[:, c, :],
-                    in_=wo_grouped[:, c],
-                )
 
-        shifted = {}
+        def copy_wo(n):
+            wo_grouped = per_unit.tile([P, 2 * P * PACK], BF16, align_bytes=64)
+            nc.scalar.copy(
+                out=wo_grouped[:].bitcast(F32).rearrange("p (a e u) -> p a e u", a=2, u=PAIRS),
+                in_=wo_banks[n][:].rearrange("p (a u) e -> p a e u", u=PAIRS),
+            )
+            wo_pieces[n] = wo_grouped
+
+        def quantise_wo(n):
+            c, first = n // PACK, (n % PACK) * 2 * P
+            nc.vector.quantize_mx(
+                out=wo_codes[:, c, first : first + 2 * P].bitcast(FP8X4),
+                scales=wo_scales[:, c, first : first + 2 * P],
+                in_=wo_pieces[n][:],
+            )
+
+        negated_scores = {}
+        bank_minima = {}
+        shifts = {}
         exponentials = {}
-        flipped = {}
+        row_sums = {}
+        divisors = {}
         weights = {}
+        flipped = {}
         grouped = {}
         coded = {}
+        sums = {}
 
-        def scores(w):
+        def scores(w, g):
             b, h, t = unit_of(w)
             k_t = key_tiles[b * H + h]
-            negated = per_unit.tile([P, J], F32)
-            bank_min = columns.tile([P, KEY_PASSES], F32)
-            for g in range(KEY_PASSES):
-                s_bank = psum_scores.tile([P, K_PASS], F32)
-                nc.tensor.matmul(
-                    out=s_bank[:],
-                    lhsT=q_t[:, b, h * Q_TILES + t, :],
-                    rhs=k_t[:, g * PACK : (g + 1) * PACK, :].rearrange("d x p -> d (x p)"),
-                    start=True,
-                    stop=True,
-                )
-                nc.vector.tensor_scalar(
-                    out=negated[:, g * K_PASS : (g + 1) * K_PASS],
-                    in0=s_bank[:],
-                    scalar1=-SCALE,
-                    scalar2=None,
-                    op0=ALU.mult,
-                    op1=ALU.min,
-                    accum_out=bank_min[:, g : g + 1],
-                )
+            if g == 0:
+                negated = per_unit.tile([P, J], F32)
+                bank_min = columns.tile([P, KEY_PASSES], F32)
+                negated_scores[w] = negated
+                bank_minima[w] = bank_min
+            s_bank = psum_scores.tile([P, K_PASS], F32)
+            nc.tensor.matmul(
+                out=s_bank[:],
+                lhsT=q_t[:, b, h * Q_TILES + t, :],
+                rhs=k_t[:, g * PACK : (g + 1) * PACK, :].rearrange("d x p -> d (x p)"),
+                start=True,
+                stop=True,
+            )
+            nc.vector.tensor_scalar(
+                out=negated_scores[w][:, g * K_PASS : (g + 1) * K_PASS],
+                in0=s_bank[:],
+                scalar1=-SCALE,
+                scalar2=None,
+                op0=ALU.mult,
+                op1=ALU.min,
+                accum_out=bank_minima[w][:, g : g + 1],
+            )
+
+        def row_shift(w):
             shift = columns.tile([P, 1], F32)
-            nc.vector.tensor_reduce(out=shift[:], in_=bank_min[:], axis=AXIS.X, op=ALU.min)
-            shifted[w] = (negated, shift)
+            nc.vector.tensor_reduce(out=shift[:], in_=bank_minima[w][:], axis=AXIS.X, op=ALU.min)
+            shifts[w] = shift
 
         def exponential(w):
-            negated, shift = shifted[w]
             e = per_unit.tile([P, J], BF16)
             row_sum = columns.tile([P, 1], F32)
             nc.scalar.activation(
-                out=e[:], in_=negated[:], func=ACT.Exp, bias=shift[:], scale=-1.0, accum_out=row_sum[:]
+                out=e[:], in_=negated_scores[w][:], func=ACT.Exp, bias=shifts[w][:], scale=-1.0, accum_out=row_sum[:]
             )
-            exponentials[w] = (e, row_sum)
+            exponentials[w] = e
+            row_sums[w] = row_sum
 
-        def row_weight(w):
-            h = unit_of(w)[1]
-            inverse = columns.tile([P, 1], F32)
-            nc.vector.reciprocal(out=inverse[:], in_=exponentials[w][1][:])
-            weight = columns.tile([P, 1], F32)
-            nc.vector.tensor_mul(out=weight[:], in0=inverse[:], in1=g_retrieved[:, h : h + 1])
-            weights[w] = weight
+        def row_divisor(w):
+            b, h, t = unit_of(w)
+            if t == 0:
+                divisor = columns.tile([P, Q_TILES], F32)
+                divisors[b * H + h] = divisor
+            nc.gpsimd.tensor_scalar(
+                out=divisors[b * H + h][:, t : t + 1],
+                in0=row_sums[w][:],
+                scalar1=retrieved_divisor[:, h : h + 1],
+                scalar2=0.0,
+                op0=ALU.mult,
+                op1=ALU.add,
+            )
 
-        def flip_exponentials(w):
-            words = exponentials[w][0][:].bitcast(F32)
-            flipped[w] = [
-                flip_words([words[:, (first + n) * P : (first + n + 1) * P] for n in range(BANK_WORD_BLOCKS)])
-                for first in range(0, KEY_PASSES * PAIRS, BANK_WORD_BLOCKS)
-            ]
+        def row_weights(number):
+            weight = columns.tile([P, Q_TILES], F32)
+            nc.vector.reciprocal(out=weight[:], in_=divisors[number][:])
+            weights[number] = weight
 
-        def group_exponentials(w):
-            e_grouped = per_unit.tile([P, KEY_PASSES * P * PACK], BF16, align_bytes=64)
-            words = e_grouped[:].bitcast(F32).rearrange("p (g r u) -> p g r u", g=KEY_PASSES, u=PAIRS)
-            for n, bank in enumerate(flipped[w]):
-                nc.scalar.copy(
-                    out=words[:, n * PASSES_IN_BANK : (n + 1) * PASSES_IN_BANK],
-                    in_=bank[:].rearrange("p (g u) r -> p g r u", u=PAIRS),
-                )
-            grouped[w] = e_grouped
+        def flip_exponentials(w, n):
+            words = exponentials[w][:].bitcast(F32)
+            first = n * BANK_WORD_BLOCKS
+            flipped[(w, n)] = flip_words([words[:, (first + m) * P : (first + m + 1) * P] for m in range(BANK_WORD_BLOCKS)])
+
+        def group_exponentials(w, n):
+            if n == 0:
+                e_grouped = per_unit.tile([P, KEY_PASSES * P * PACK], BF16, align_bytes=64)
+                grouped[w] = e_grouped
+            words = grouped[w][:].bitcast(F32).rearrange("p (g r u) -> p g r u", g=KEY_PASSES, u=PAIRS)
+            nc.scalar.copy(
+                out=words[:, n * PASSES_IN_BANK : (n + 1) * PASSES_IN_BANK],
+                in_=flipped[(w, n)][:].rearrange("p (g u) r -> p g r u", u=PAIRS),
+            )
 
         def quantise_exponentials(w):
             e_codes = per_unit.tile([P, KEY_PASSES * P], U32, align_bytes=64)
@@ -284,7 +331,7 @@ def tile_knnxlmultiheadsattention_pb_kernel(tc, q, qkv, kv_external, gate, Wo, b
             )
             coded[w] = (e_codes, e_scales)
 
-        def multiply_and_fuse(w):
+        def multiply(w):
             b, h, t = unit_of(w)
             e_codes, e_scales = coded[w]
             v_codes, v_scales = value_tiles[b * H + h]
@@ -299,84 +346,129 @@ def tile_knnxlmultiheadsattention_pb_kernel(tc, q, qkv, kv_external, gate, Wo, b
                     start=(g == 0),
                     stop=(g == KEY_PASSES - 1),
                 )
+            sums[w] = retrieved
+
+        def fuse(w):
+            b, h, t = unit_of(w)
             nc.vector.scalar_tensor_tensor(
                 out=merged[b][t][:, h * D : (h + 1) * D],
-                in0=retrieved[:],
-                scalar=weights[w][:],
+                in0=sums[w][:],
+                scalar=weights[b * H + h][:, t : t + 1],
                 in1=local_part[:, b, h * Q_TILES + t, :],
                 op0=ALU.mult,
                 op1=ALU.add,
             )
 
-        merged_grouped = {}
+        merged_banks = {}
+        merged_codes = {}
 
-        def group_merged(b, t):
+        def flip_merged(b, t, c):
             words = merged[b][t][:].bitcast(F32)
-            bank = flip_words(
-                [words[:, c * K_WORDS + u : (c + 1) * K_WORDS : PAIRS] for c in range(HD_PASSES) for u in range(PAIRS)]
+            merged_banks[(b, t, c)] = flip_words(
+                [words[:, c * K_WORDS + u : (c + 1) * K_WORDS : PAIRS] for u in range(PAIRS)]
             )
-            m_grouped = per_unit.tile([P, HD_PASSES * P * PACK], BF16, align_bytes=64)
-            nc.scalar.copy(
-                out=m_grouped[:].bitcast(F32).rearrange("p (c r u) -> p c r u", c=HD_PASSES, u=PAIRS),
-                in_=bank[:].rearrange("p (c u) r -> p c r u", u=PAIRS),
-            )
-            merged_grouped[(b, t)] = m_grouped
 
-        def project(b, t):
-            m_grouped = merged_grouped[(b, t)]
-            m_codes = per_unit.tile([P, HD_PASSES * P], U32, align_bytes=64)
-            m_scales = per_unit.tile([P, HD_PASSES * P], U8, align_bytes=64)
-            nc.vector.quantize_mx(
-                out=m_codes[:].bitcast(FP8X4),
-                scales=m_scales[:],
-                in_=m_grouped[:],
+        merged_words = {}
+
+        def copy_merged(b, t, c):
+            m_grouped = per_unit.tile([P, P * PACK], BF16, align_bytes=64)
+            nc.scalar.copy(
+                out=m_grouped[:].bitcast(F32).rearrange("p (r u) -> p r u", u=PAIRS),
+                in_=merged_banks[(b, t, c)][:, :PAIRS, :].rearrange("p u r -> p r u"),
             )
-            for first in range(0, E, N_OUT):
-                projected = psum_mx.tile([P, N_OUT], F32, tag="sums")
-                for c in range(HD_PASSES):
-                    nc.tensor.matmul_mx(
-                        out=projected[:],
-                        lhsT=m_codes[:, c * P : (c + 1) * P].bitcast(FP8X4),
-                        lhsT_scale=m_scales[:, c * P : (c + 1) * P],
-                        rhs=wo_codes[:, c, first : first + N_OUT].bitcast(FP8X4),
-                        rhs_scale=wo_scales[:, c, first : first + N_OUT],
-                        start=(c == 0),
-                        stop=(c == HD_PASSES - 1),
-                    )
-                result = per_unit.tile([P, N_OUT], F32)
-                nc.vector.tensor_tensor(
-                    out=result[:], in0=projected[:], in1=bias_rows[:, first : first + N_OUT], op=ALU.add
+            merged_words[(b, t, c)] = m_grouped
+
+        def quantise_merged(b, t, c):
+            m_codes = merged_code_pool.tile([P, P], U32, align_bytes=64)
+            m_scales = merged_code_pool.tile([P, P], U8, align_bytes=64)
+            nc.vector.quantize_mx(out=m_codes[:].bitcast(FP8X4), scales=m_scales[:], in_=merged_words[(b, t, c)][:])
+            merged_codes[(b, t, c)] = (m_codes, m_scales)
+
+        def project(b, t, n):
+            cols = slice(n * N_OUT, (n + 1) * N_OUT)
+            projected = psum_flip.tile([P, N_OUT], F32, tag="flip")
+            for c in range(HD_PASSES):
+                m_codes, m_scales = merged_codes[(b, t, c)]
+                nc.tensor.matmul_mx(
+                    out=projected[:],
+                    lhsT=m_codes[:].bitcast(FP8X4),
+                    lhsT_scale=m_scales[:],
+                    rhs=wo_codes[:, c, cols].bitcast(FP8X4),
+                    rhs_scale=wo_scales[:, c, cols],
+                    start=(c == 0),
+                    stop=(c == HD_PASSES - 1),
                 )
-                nc.sync.dma_start(out=out[b, t * P : (t + 1) * P, first : first + N_OUT], in_=result[:])
+            result = results.tile([P, N_OUT], F32)
+            nc.vector.tensor_tensor(out=result[:], in0=projected[:], in1=bias_rows[:, cols], op=ALU.add)
+            nc.sync.dma_start(out=out[b, t * P : (t + 1) * P, cols], in_=result[:])
 
         def is_unit(w):
             return 0 <= w < UNITS
 
-        def closes_merged(w):
-            return is_unit(w) and unit_of(w)[1] == H - 1
+        def merged_half(w):
+            if not is_unit(w):
+                return None
+            b, h, t = unit_of(w)
+            return (b, t, h // PACK) if h % PACK == PACK - 1 else None
 
-        for step in range(KEY_LEAD - 1):
-            prepare_keys(step)
-        for r in range(-1, UNITS + 4):
-            if is_unit(r - 2):
-                quantise_exponentials(r - 2)
-            if is_unit(r + 1):
-                scores(r + 1)
+        prepare_queries(0)
+        for half in range(2):
+            regroup_values(0, half)
+        for g in range(KEY_PASSES):
+            flip_keys(0, [g])
+            copy_keys(0, [g], nc.vector.tensor_copy if g % 2 == 0 else nc.scalar.copy)
+            if g > 0:
+                scores(0, g - 1)
+        scores(0, KEY_PASSES - 1)
+        row_shift(0)
+        for r in range(-1, UNITS + 8):
+            new, flat, code = r + 1, r - 1, r - 2
+            keys = key_step(r + KEY_LEAD)
+            wo_step, wo_rest = divmod(r - WO_START, 2)
+            if is_unit(r - 3):
+                fuse(r - 3)
+            if is_unit(code):
+                quantise_exponentials(code)
+            if is_unit(r):
+                quantise_values(r // 2, r % 2)
+                regroup_values(r // 2 + 1, r % 2)
+            if is_unit(new) and new > 0:
+                for g in range(KEY_PASSES):
+                    scores(new, g)
+                row_shift(new)
             if is_unit(r):
                 exponential(r)
-            if is_unit(r - 1):
-                flip_exponentials(r - 1)
-            if is_unit(r - 2):
-                multiply_and_fuse(r - 2)
-            if closes_merged(r - 3):
-                project(unit_of(r - 3)[0], unit_of(r - 3)[2])
-            if is_unit(r - 1):
-                row_weight(r - 1)
-            if is_unit(r - 1):
-                group_exponentials(r - 1)
-            prepare_keys(r + KEY_LEAD)
-            prepare_values(r + VALUE_LEAD)
-            if UNITS // 4 <= r < UNITS // 2:
-                prepare_wo(r - UNITS // 4)
-            if closes_merged(r - 2):
-                group_merged(unit_of(r - 2)[0], unit_of(r - 2)[2])
+            if is_unit(flat):
+                flip_exponentials(flat, 0)
+                flip_exponentials(flat, 1)
+            if is_unit(code):
+                multiply(code)
+            if r == 0:
+                prepare_gates()
+            if is_unit(r) and r % 2 == 0:
+                weigh_local(r // 2)
+            if is_unit(flat):
+                row_divisor(flat)
+                if flat % Q_TILES == Q_TILES - 1:
+                    row_weights(flat // Q_TILES)
+                group_exponentials(flat, 0)
+                group_exponentials(flat, 1)
+            if keys:
+                flip_keys(*keys)
+                copy_keys(*keys, nc.scalar.copy)
+            if r % (PAIR * Q_TILES) == (-QUERY_LEAD) % (PAIR * Q_TILES) and is_unit(r + QUERY_LEAD):
+                prepare_queries((r + QUERY_LEAD) // (PAIR * Q_TILES))
+            if 0 <= wo_step < WO_PIECES and wo_rest == 0:
+                flip_wo(wo_step)
+                copy_wo(wo_step)
+            if 0 <= wo_step < WO_PIECES and wo_rest == 1:
+                quantise_wo(wo_step)
+            if merged_half(r - 4):
+                flip_merged(*merged_half(r - 4))
+                copy_merged(*merged_half(r - 4))
+            if merged_half(r - 5):
+                quantise_merged(*merged_half(r - 5))
+            for n in range(E // N_OUT):
+                for t in range(Q_TILES):
+                    if merged_half(r - 6 - n - t) == ((r - 6 - n - t) // (H * Q_TILES), t, HD_PASSES - 1):
+                        project((r - 6 - n - t) // (H * Q_TILES), t, n)

@@ -34,6 +34,8 @@ UNITS = B * H * Q_TILES
 HEAD_STEPS = 2
 KEY_LEAD = 3
 QUERY_LEAD = 3
+TAIL_W = 3
+WARM_UP = 9
 WO_PIECES = 8
 WO_START = 4
 
@@ -79,6 +81,10 @@ def tile_knnxlmultiheadsattention_pb_kernel(tc, q, qkv, kv_external, gate, Wo, b
             for n, block in enumerate(blocks):
                 nc.tensor.transpose(bank[:, n, :], block, ident_words[:])
             return bank
+
+        def keep_clock(pool, tag):
+            unread = pool.tile([P, P], F32, tag=tag)
+            nc.tensor.matmul(out=unread[:], lhsT=ident_words[:], rhs=ident_words[:], start=True, stop=True)
 
         def unit_of(w):
             return w // (H * Q_TILES), (w % (H * Q_TILES)) // Q_TILES, w % Q_TILES
@@ -255,7 +261,7 @@ def tile_knnxlmultiheadsattention_pb_kernel(tc, q, qkv, kv_external, gate, Wo, b
                 bank_min = columns.tile([P, KEY_PASSES], F32)
                 negated_scores[w] = negated
                 bank_minima[w] = bank_min
-            s_bank = psum_scores.tile([P, K_PASS], F32)
+            s_bank = psum_scores.tile([P, K_PASS], F32, tag="scores")
             nc.tensor.matmul(
                 out=s_bank[:],
                 lhsT=q_t[:, b, h * Q_TILES + t, :],
@@ -331,11 +337,11 @@ def tile_knnxlmultiheadsattention_pb_kernel(tc, q, qkv, kv_external, gate, Wo, b
             )
             coded[w] = (e_codes, e_scales)
 
-        def multiply(w):
+        def multiply(w, pool, tag):
             b, h, t = unit_of(w)
             e_codes, e_scales = coded[w]
             v_codes, v_scales = value_tiles[b * H + h]
-            retrieved = psum_mx.tile([P, D], F32, tag="sums")
+            retrieved = pool.tile([P, D], F32, tag=tag)
             for g in range(KEY_PASSES):
                 nc.tensor.matmul_mx(
                     out=retrieved[:],
@@ -411,6 +417,8 @@ def tile_knnxlmultiheadsattention_pb_kernel(tc, q, qkv, kv_external, gate, Wo, b
             b, h, t = unit_of(w)
             return (b, t, h // PACK) if h % PACK == PACK - 1 else None
 
+        for n in range(WARM_UP):
+            keep_clock(psum_scores, "scores")
         prepare_queries(0)
         for half in range(2):
             regroup_values(0, half)
@@ -419,14 +427,16 @@ def tile_knnxlmultiheadsattention_pb_kernel(tc, q, qkv, kv_external, gate, Wo, b
             copy_keys(0, [g], nc.vector.tensor_copy if g % 2 == 0 else nc.scalar.copy)
             if g > 0:
                 scores(0, g - 1)
+            else:
+                keep_clock(psum_mx, "sums")
         scores(0, KEY_PASSES - 1)
         row_shift(0)
-        for r in range(-1, UNITS + 8):
-            new, flat, code = r + 1, r - 1, r - 2
+        for r in range(-1, UNITS):
+            new, flat, code, done = r + 1, r - 1, r - 2, r - 3
             keys = key_step(r + KEY_LEAD)
             wo_step, wo_rest = divmod(r - WO_START, 2)
-            if is_unit(r - 3):
-                fuse(r - 3)
+            if is_unit(done):
+                fuse(done)
             if is_unit(code):
                 quantise_exponentials(code)
             if is_unit(r):
@@ -436,28 +446,33 @@ def tile_knnxlmultiheadsattention_pb_kernel(tc, q, qkv, kv_external, gate, Wo, b
                 for g in range(KEY_PASSES):
                     scores(new, g)
                 row_shift(new)
-            if is_unit(r):
+            if is_unit(r) and is_unit(new):
                 exponential(r)
             if is_unit(flat):
                 flip_exponentials(flat, 0)
                 flip_exponentials(flat, 1)
+            if keys:
+                flip_keys(*keys)
+            if is_unit(r):
+                keep_clock(psum_mx, "sums")
             if is_unit(code):
-                multiply(code)
-            if r == 0:
-                prepare_gates()
-            if is_unit(r) and r % 2 == 0:
-                weigh_local(r // 2)
+                multiply(code, psum_mx, "sums")
             if is_unit(flat):
                 row_divisor(flat)
                 if flat % Q_TILES == Q_TILES - 1:
                     row_weights(flat // Q_TILES)
                 group_exponentials(flat, 0)
                 group_exponentials(flat, 1)
+            if not is_unit(new):
+                exponential(r)
             if keys:
-                flip_keys(*keys)
-                copy_keys(*keys, nc.scalar.copy)
-            if r % (PAIR * Q_TILES) == (-QUERY_LEAD) % (PAIR * Q_TILES) and is_unit(r + QUERY_LEAD):
-                prepare_queries((r + QUERY_LEAD) // (PAIR * Q_TILES))
+                copy_keys(*keys, nc.scalar.copy if is_unit(r) else nc.vector.tensor_copy)
+            if r == 0:
+                prepare_gates()
+            if is_unit(r) and r % 2 == 0:
+                weigh_local(r // 2)
+            if r % PAIR_BLOCKS == (-QUERY_LEAD) % PAIR_BLOCKS and is_unit(r + QUERY_LEAD):
+                prepare_queries((r + QUERY_LEAD) // PAIR_BLOCKS)
             if 0 <= wo_step < WO_PIECES and wo_rest == 0:
                 flip_wo(wo_step)
                 copy_wo(wo_step)
@@ -468,7 +483,36 @@ def tile_knnxlmultiheadsattention_pb_kernel(tc, q, qkv, kv_external, gate, Wo, b
                 copy_merged(*merged_half(r - 4))
             if merged_half(r - 5):
                 quantise_merged(*merged_half(r - 5))
-            for n in range(E // N_OUT):
-                for t in range(Q_TILES):
-                    if merged_half(r - 6 - n - t) == ((r - 6 - n - t) // (H * Q_TILES), t, HD_PASSES - 1):
-                        project((r - 6 - n - t) // (H * Q_TILES), t, n)
+            for t in range(Q_TILES):
+                for n in range(E // N_OUT):
+                    if r - 6 - n - t == H * Q_TILES - Q_TILES + t:
+                        project(0, t, n)
+
+        before, last = UNITS - 2, UNITS - 1
+        fuse(before - 1)
+        quantise_exponentials(before)
+        for n in range(TAIL_W):
+            keep_clock(psum_scores, "scores")
+        multiply(before, psum_scores, "scores")
+        flip_exponentials(last, 0)
+        flip_exponentials(last, 1)
+        row_divisor(last)
+        row_weights(last // Q_TILES)
+        group_exponentials(last, 0)
+        group_exponentials(last, 1)
+        fuse(before)
+        quantise_exponentials(last)
+        flip_merged(*merged_half(before))
+        for n in range(TAIL_W):
+            keep_clock(psum_scores, "scores")
+        multiply(last, psum_scores, "scores")
+        copy_merged(*merged_half(before))
+        quantise_merged(*merged_half(before))
+        fuse(last)
+        for n in range(E // N_OUT):
+            project(*merged_half(before)[:2], n)
+        flip_merged(*merged_half(last))
+        copy_merged(*merged_half(last))
+        quantise_merged(*merged_half(last))
+        for n in range(E // N_OUT):
+            project(*merged_half(last)[:2], n)

@@ -33,8 +33,8 @@ SCALE = D**-0.5
 UNITS = B * H * Q_TILES
 HEAD_STEPS = 2
 KEY_LEAD = 3
-QUERY_LEAD = 3
-TAIL_W = 3
+QUERY_LEAD = 2
+TAIL_W = 2
 WARM_UP = 9
 WO_PIECES = 8
 WO_START = 4
@@ -133,6 +133,8 @@ def tile_knnxlmultiheadsattention_pb_kernel(tc, q, qkv, kv_external, gate, Wo, b
 
         q_t = keep.tile([P, B, H * Q_TILES, P], BF16)
         local_part = keep.tile([P, B, H * Q_TILES, D], F32)
+        minus_one = keep.tile([P, Q_TILES], F32)
+        nc.gpsimd.memset(minus_one[:], -1.0)
         merged = [
             [keep.tile([P, HD], BF16, name="merged_%d_%d" % (b, t)) for t in range(Q_TILES)] for b in range(B)
         ]
@@ -142,11 +144,19 @@ def tile_knnxlmultiheadsattention_pb_kernel(tc, q, qkv, kv_external, gate, Wo, b
         key_tiles = {}
         value_tiles = {}
 
-        def prepare_queries(n):
+        query_banks = {}
+
+        def query_blocks(n):
             b, first = n // (H // PAIR), (n % (H // PAIR)) * PAIR_BLOCKS
-            blocks = slice(first, first + PAIR_BLOCKS)
-            bank = flip([q_raw[:, b, first + m, :] for m in range(PAIR_BLOCKS)])
-            nc.vector.tensor_copy(out=q_t[:, b, blocks, :], in_=bank[:, :PAIR_BLOCKS, :])
+            return b, slice(first, first + PAIR_BLOCKS)
+
+        def flip_queries(n):
+            b, blocks = query_blocks(n)
+            query_banks[n] = flip([q_raw[:, b, m, :] for m in range(blocks.start, blocks.stop)])
+
+        def copy_queries(n):
+            b, blocks = query_blocks(n)
+            nc.vector.tensor_copy(out=q_t[:, b, blocks, :], in_=query_banks[n][:, :PAIR_BLOCKS, :])
 
         key_banks = {}
 
@@ -284,14 +294,21 @@ def tile_knnxlmultiheadsattention_pb_kernel(tc, q, qkv, kv_external, gate, Wo, b
             nc.vector.tensor_reduce(out=shift[:], in_=bank_minima[w][:], axis=AXIS.X, op=ALU.min)
             shifts[w] = shift
 
-        def exponential(w):
-            e = per_unit.tile([P, J], BF16)
-            row_sum = columns.tile([P, 1], F32)
+        def exponential(w, first=0, count=KEY_PASSES):
+            if first == 0:
+                e = per_unit.tile([P, J], BF16)
+                row_sum = columns.tile([P, KEY_PASSES], F32)
+                exponentials[w] = e
+                row_sums[w] = row_sum
+            cols = slice(first * K_PASS, (first + count) * K_PASS)
             nc.scalar.activation(
-                out=e[:], in_=negated_scores[w][:], func=ACT.Exp, bias=shifts[w][:], scale=-1.0, accum_out=row_sum[:]
+                out=exponentials[w][:, cols],
+                in_=negated_scores[w][:, cols],
+                func=ACT.Exp,
+                bias=shifts[w][:],
+                scale=-1.0,
+                accum_out=row_sums[w][:, first : first + 1],
             )
-            exponentials[w] = e
-            row_sums[w] = row_sum
 
         def row_divisor(w):
             b, h, t = unit_of(w)
@@ -300,51 +317,61 @@ def tile_knnxlmultiheadsattention_pb_kernel(tc, q, qkv, kv_external, gate, Wo, b
                 divisors[b * H + h] = divisor
             nc.gpsimd.tensor_scalar(
                 out=divisors[b * H + h][:, t : t + 1],
-                in0=row_sums[w][:],
+                in0=row_sums[w][:, :1],
                 scalar1=retrieved_divisor[:, h : h + 1],
                 scalar2=0.0,
                 op0=ALU.mult,
                 op1=ALU.add,
             )
 
-        def row_weights(number):
-            weight = columns.tile([P, Q_TILES], F32)
-            nc.vector.reciprocal(out=weight[:], in_=divisors[number][:])
-            weights[number] = weight
+        def row_weights(number, t=None):
+            if number not in weights:
+                weight = columns.tile([P, Q_TILES], F32)
+                weights[number] = weight
+            cols = slice(0, Q_TILES) if t is None else slice(t, t + 1)
+            nc.gpsimd.tensor_tensor(
+                out=weights[number][:, cols], in0=divisors[number][:, cols], in1=minus_one[:, cols], op=ALU.pow
+            )
 
-        def flip_exponentials(w, n):
+        def flip_exponentials(w, first, count):
             words = exponentials[w][:].bitcast(F32)
-            first = n * BANK_WORD_BLOCKS
-            flipped[(w, n)] = flip_words([words[:, (first + m) * P : (first + m + 1) * P] for m in range(BANK_WORD_BLOCKS)])
+            flipped[(w, first)] = flip_words(
+                [words[:, n * P : (n + 1) * P] for n in range(first * PAIRS, (first + count) * PAIRS)]
+            )
 
-        def group_exponentials(w, n):
-            if n == 0:
+        def group_exponentials(w, first, count):
+            if first == 0:
                 e_grouped = per_unit.tile([P, KEY_PASSES * P * PACK], BF16, align_bytes=64)
                 grouped[w] = e_grouped
             words = grouped[w][:].bitcast(F32).rearrange("p (g r u) -> p g r u", g=KEY_PASSES, u=PAIRS)
             nc.scalar.copy(
-                out=words[:, n * PASSES_IN_BANK : (n + 1) * PASSES_IN_BANK],
-                in_=flipped[(w, n)][:].rearrange("p (g u) r -> p g r u", u=PAIRS),
+                out=words[:, first : first + count],
+                in_=flipped[(w, first)][:, : count * PAIRS, :].rearrange("p (g u) r -> p g r u", u=PAIRS),
             )
 
-        def quantise_exponentials(w):
-            e_codes = per_unit.tile([P, KEY_PASSES * P], U32, align_bytes=64)
-            e_scales = per_unit.tile([P, KEY_PASSES * P], U8, align_bytes=64)
+        def quantise_exponentials(w, first=0, count=KEY_PASSES):
+            if first == 0:
+                e_codes = per_unit.tile([P, KEY_PASSES * P], U32, align_bytes=64)
+                e_scales = per_unit.tile([P, KEY_PASSES * P], U8, align_bytes=64)
+                coded[w] = (e_codes, e_scales)
+            e_codes, e_scales = coded[w]
+            cols = slice(first * P, (first + count) * P)
             nc.vector.quantize_mx(
-                out=e_codes[:].bitcast(FP8X4),
-                scales=e_scales[:],
-                in_=grouped[w][:],
+                out=e_codes[:, cols].bitcast(FP8X4),
+                scales=e_scales[:, cols],
+                in_=grouped[w][:, first * P * PACK : (first + count) * P * PACK],
             )
-            coded[w] = (e_codes, e_scales)
 
-        def multiply(w, pool, tag):
+        def multiply(w, pool, tag, first=0, count=KEY_PASSES):
             b, h, t = unit_of(w)
             e_codes, e_scales = coded[w]
             v_codes, v_scales = value_tiles[b * H + h]
-            retrieved = pool.tile([P, D], F32, tag=tag)
-            for g in range(KEY_PASSES):
+            if first == 0:
+                retrieved = pool.tile([P, D], F32, tag=tag)
+                sums[w] = retrieved
+            for g in range(first, first + count):
                 nc.tensor.matmul_mx(
-                    out=retrieved[:],
+                    out=sums[w][:],
                     lhsT=e_codes[:, g * P : (g + 1) * P].bitcast(FP8X4),
                     lhsT_scale=e_scales[:, g * P : (g + 1) * P],
                     rhs=v_codes[:, g * D : (g + 1) * D].bitcast(FP8X4),
@@ -352,7 +379,6 @@ def tile_knnxlmultiheadsattention_pb_kernel(tc, q, qkv, kv_external, gate, Wo, b
                     start=(g == 0),
                     stop=(g == KEY_PASSES - 1),
                 )
-            sums[w] = retrieved
 
         def fuse(w):
             b, h, t = unit_of(w)
@@ -419,7 +445,8 @@ def tile_knnxlmultiheadsattention_pb_kernel(tc, q, qkv, kv_external, gate, Wo, b
 
         for n in range(WARM_UP):
             keep_clock(psum_scores, "scores")
-        prepare_queries(0)
+        flip_queries(0)
+        copy_queries(0)
         for half in range(2):
             regroup_values(0, half)
         for g in range(KEY_PASSES):
@@ -435,6 +462,7 @@ def tile_knnxlmultiheadsattention_pb_kernel(tc, q, qkv, kv_external, gate, Wo, b
             new, flat, code, done = r + 1, r - 1, r - 2, r - 3
             keys = key_step(r + KEY_LEAD)
             wo_step, wo_rest = divmod(r - WO_START, 2)
+            queries, queries_rest = divmod(r + QUERY_LEAD, PAIR_BLOCKS)
             if is_unit(done):
                 fuse(done)
             if is_unit(code):
@@ -442,47 +470,51 @@ def tile_knnxlmultiheadsattention_pb_kernel(tc, q, qkv, kv_external, gate, Wo, b
             if is_unit(r):
                 quantise_values(r // 2, r % 2)
                 regroup_values(r // 2 + 1, r % 2)
+            if queries_rest == 0 and 0 < queries < B * H // PAIR:
+                flip_queries(queries)
+                copy_queries(queries)
             if is_unit(new) and new > 0:
                 for g in range(KEY_PASSES):
                     scores(new, g)
+            if r == 1:
+                prepare_gates()
+            if is_unit(flat):
+                row_divisor(flat)
+                if flat % Q_TILES == Q_TILES - 1:
+                    row_weights(flat // Q_TILES)
+            if 0 <= wo_step < WO_PIECES and wo_rest == 1:
+                quantise_wo(wo_step)
+            if merged_half(r - 5):
+                quantise_merged(*merged_half(r - 5))
+            if is_unit(new) and new > 0:
                 row_shift(new)
             if is_unit(r) and is_unit(new):
                 exponential(r)
             if is_unit(flat):
-                flip_exponentials(flat, 0)
-                flip_exponentials(flat, 1)
+                for first in range(0, KEY_PASSES, PASSES_IN_BANK):
+                    flip_exponentials(flat, first, PASSES_IN_BANK)
             if keys:
                 flip_keys(*keys)
             if is_unit(r):
                 keep_clock(psum_mx, "sums")
             if is_unit(code):
                 multiply(code, psum_mx, "sums")
+            if is_unit(r) and r % Q_TILES == Q_TILES - 1:
+                weigh_local(r // Q_TILES)
             if is_unit(flat):
-                row_divisor(flat)
-                if flat % Q_TILES == Q_TILES - 1:
-                    row_weights(flat // Q_TILES)
-                group_exponentials(flat, 0)
-                group_exponentials(flat, 1)
+                for first in range(0, KEY_PASSES, PASSES_IN_BANK):
+                    group_exponentials(flat, first, PASSES_IN_BANK)
             if not is_unit(new):
-                exponential(r)
+                for g in range(KEY_PASSES):
+                    exponential(r, g, 1)
             if keys:
                 copy_keys(*keys, nc.scalar.copy if is_unit(r) else nc.vector.tensor_copy)
-            if r == 0:
-                prepare_gates()
-            if is_unit(r) and r % 2 == 0:
-                weigh_local(r // 2)
-            if r % PAIR_BLOCKS == (-QUERY_LEAD) % PAIR_BLOCKS and is_unit(r + QUERY_LEAD):
-                prepare_queries((r + QUERY_LEAD) // PAIR_BLOCKS)
             if 0 <= wo_step < WO_PIECES and wo_rest == 0:
                 flip_wo(wo_step)
                 copy_wo(wo_step)
-            if 0 <= wo_step < WO_PIECES and wo_rest == 1:
-                quantise_wo(wo_step)
             if merged_half(r - 4):
                 flip_merged(*merged_half(r - 4))
                 copy_merged(*merged_half(r - 4))
-            if merged_half(r - 5):
-                quantise_merged(*merged_half(r - 5))
             for t in range(Q_TILES):
                 for n in range(E // N_OUT):
                     if r - 6 - n - t == H * Q_TILES - Q_TILES + t:
@@ -491,22 +523,33 @@ def tile_knnxlmultiheadsattention_pb_kernel(tc, q, qkv, kv_external, gate, Wo, b
         before, last = UNITS - 2, UNITS - 1
         fuse(before - 1)
         quantise_exponentials(before)
-        for n in range(TAIL_W):
-            keep_clock(psum_scores, "scores")
+        for g in range(2):
+            flip_exponentials(last, g, 1)
+            group_exponentials(last, g, 1)
         multiply(before, psum_scores, "scores")
-        flip_exponentials(last, 0)
-        flip_exponentials(last, 1)
-        row_divisor(last)
-        row_weights(last // Q_TILES)
-        group_exponentials(last, 0)
-        group_exponentials(last, 1)
+        for g in range(2, KEY_PASSES):
+            flip_exponentials(last, g, 1)
+            group_exponentials(last, g, 1)
+        row_weights(last // Q_TILES, 0)
         fuse(before)
-        quantise_exponentials(last)
+        sum_parts = columns.tile([P, KEY_PASSES], F32)
+        nc.vector.tensor_scalar(
+            out=sum_parts[:],
+            in0=row_sums[last][:],
+            scalar1=retrieved_divisor[:, H - 1 :],
+            scalar2=None,
+            op0=ALU.mult,
+            op1=ALU.add,
+            accum_out=divisors[last // Q_TILES][:, Q_TILES - 1 :],
+        )
+        row_weights(last // Q_TILES, 1)
         flip_merged(*merged_half(before))
+        copy_merged(*merged_half(before))
         for n in range(TAIL_W):
             keep_clock(psum_scores, "scores")
-        multiply(last, psum_scores, "scores")
-        copy_merged(*merged_half(before))
+        for g in range(KEY_PASSES):
+            quantise_exponentials(last, g, 1)
+            multiply(last, psum_scores, "scores", g, 1)
         quantise_merged(*merged_half(before))
         fuse(last)
         for n in range(E // N_OUT):

@@ -34,7 +34,7 @@ UNITS = B * H * Q_TILES
 HEAD_STEPS = 2
 KEY_LEAD = 3
 QUERY_LEAD = 2
-TAIL_W = 2
+TAIL_W = 1
 WARM_UP = 9
 WO_PIECES = 8
 WO_START = 4
@@ -90,6 +90,9 @@ def tile_knnxlmultiheadsattention_pb_kernel(tc, q, qkv, kv_external, gate, Wo, b
             return w // (H * Q_TILES), (w % (H * Q_TILES)) // Q_TILES, w % Q_TILES
 
         gate_rows = keep.tile([P, H], BF16)
+        ones = keep.tile([P, P], BF16)
+        nc.gpsimd.memset(gate_rows[:], 0.0)
+        nc.gpsimd.memset(ones[:], 1.0)
         q_raw = keep.tile([P, B, H * Q_TILES, D], BF16)
         qkv_raw = keep.tile([P, B, H * Q_TILES, D], BF16)
         wo_raw = keep.tile([P, E // P, HD], BF16)
@@ -111,8 +114,8 @@ def tile_knnxlmultiheadsattention_pb_kernel(tc, q, qkv, kv_external, gate, Wo, b
             nc.sync.dma_start(out=qkv_raw[:, b, blocks], in_=qkv_rows[b][:, blocks])
             pair_tiles[n] = (k_raw, v_raw)
 
+        nc.sync.dma_start(out=gate_rows[:1, :], in_=gate.rearrange("h a b -> (a b) h"))
         load_pair(0)
-        nc.sync.dma_start(out=gate_rows[:], in_=gate.rearrange("h a b -> (h a b)").partition_broadcast(P))
         load_pair(1)
         nc.sync.dma_start(out=wo_raw[:], in_=Wo.rearrange("(a p) k -> p a k", p=P))
         load_pair(2)
@@ -121,20 +124,23 @@ def tile_knnxlmultiheadsattention_pb_kernel(tc, q, qkv, kv_external, gate, Wo, b
         g_local = keep.tile([P, H], F32)
         retrieved_divisor = keep.tile([P, H], F32)
 
+        exp_minus = keep.tile([P, H], F32)
+        exp_plus = keep.tile([P, H], F32)
+
+        def exponentiate_gates():
+            gates = psum_mx.tile([P, H], F32, tag="sums")
+            nc.tensor.matmul(out=gates[:], lhsT=ones[:], rhs=gate_rows[:], start=True, stop=True)
+            nc.scalar.activation(out=exp_minus[:], in_=gates[:], func=ACT.Exp, scale=-1.0)
+            nc.scalar.activation(out=exp_plus[:], in_=gates[:], func=ACT.Exp)
+
         def prepare_gates():
-            exp_minus = keep.tile([P, H], F32)
-            exp_plus = keep.tile([P, H], F32)
             local_divisor = keep.tile([P, H], F32)
-            nc.scalar.activation(out=exp_minus[:], in_=gate_rows[:], func=ACT.Exp, scale=-1.0)
-            nc.scalar.activation(out=exp_plus[:], in_=gate_rows[:], func=ACT.Exp)
             nc.vector.tensor_scalar_add(out=local_divisor[:], in0=exp_minus[:], scalar1=1.0)
             nc.vector.tensor_scalar_add(out=retrieved_divisor[:], in0=exp_plus[:], scalar1=1.0)
             nc.vector.reciprocal(out=g_local[:], in_=local_divisor[:])
 
         q_t = keep.tile([P, B, H * Q_TILES, P], BF16)
         local_part = keep.tile([P, B, H * Q_TILES, D], F32)
-        minus_one = keep.tile([P, Q_TILES], F32)
-        nc.gpsimd.memset(minus_one[:], -1.0)
         merged = [
             [keep.tile([P, HD], BF16, name="merged_%d_%d" % (b, t)) for t in range(Q_TILES)] for b in range(B)
         ]
@@ -329,9 +335,7 @@ def tile_knnxlmultiheadsattention_pb_kernel(tc, q, qkv, kv_external, gate, Wo, b
                 weight = columns.tile([P, Q_TILES], F32)
                 weights[number] = weight
             cols = slice(0, Q_TILES) if t is None else slice(t, t + 1)
-            nc.gpsimd.tensor_tensor(
-                out=weights[number][:, cols], in0=divisors[number][:, cols], in1=minus_one[:, cols], op=ALU.pow
-            )
+            nc.vector.reciprocal(out=weights[number][:, cols], in_=divisors[number][:, cols])
 
         def flip_exponentials(w, first, count):
             words = exponentials[w][:].bitcast(F32)
@@ -447,6 +451,8 @@ def tile_knnxlmultiheadsattention_pb_kernel(tc, q, qkv, kv_external, gate, Wo, b
             keep_clock(psum_scores, "scores")
         flip_queries(0)
         copy_queries(0)
+        exponentiate_gates()
+        prepare_gates()
         for half in range(2):
             regroup_values(0, half)
         for g in range(KEY_PASSES):
@@ -476,8 +482,6 @@ def tile_knnxlmultiheadsattention_pb_kernel(tc, q, qkv, kv_external, gate, Wo, b
             if is_unit(new) and new > 0:
                 for g in range(KEY_PASSES):
                     scores(new, g)
-            if r == 1:
-                prepare_gates()
             if is_unit(flat):
                 row_divisor(flat)
                 if flat % Q_TILES == Q_TILES - 1:

@@ -35,7 +35,7 @@ HEAD_STEPS = 2
 KEY_LEAD = 3
 QUERY_LEAD = 2
 TAIL_W = 1
-WARM_UP = 9
+WARM_UP = 2
 WO_PIECES = 8
 WO_START = 4
 
@@ -91,8 +91,8 @@ def tile_knnxlmultiheadsattention_pb_kernel(tc, q, qkv, kv_external, gate, Wo, b
 
         gate_rows = keep.tile([P, H], BF16)
         ones = keep.tile([P, P], BF16)
-        nc.gpsimd.memset(gate_rows[:], 0.0)
-        nc.gpsimd.memset(ones[:], 1.0)
+        nc.vector.memset(gate_rows[:], 0.0)
+        nc.vector.memset(ones[:], 1.0)
         q_raw = keep.tile([P, B, H * Q_TILES, D], BF16)
         qkv_raw = keep.tile([P, B, H * Q_TILES, D], BF16)
         wo_raw = keep.tile([P, E // P, HD], BF16)
@@ -114,8 +114,8 @@ def tile_knnxlmultiheadsattention_pb_kernel(tc, q, qkv, kv_external, gate, Wo, b
             nc.sync.dma_start(out=qkv_raw[:, b, blocks], in_=qkv_rows[b][:, blocks])
             pair_tiles[n] = (k_raw, v_raw)
 
-        nc.sync.dma_start(out=gate_rows[:1, :], in_=gate.rearrange("h a b -> (a b) h"))
         load_pair(0)
+        nc.sync.dma_start(out=gate_rows[:1, :], in_=gate.rearrange("h a b -> (a b) h"))
         load_pair(1)
         nc.sync.dma_start(out=wo_raw[:], in_=Wo.rearrange("(a p) k -> p a k", p=P))
         load_pair(2)
@@ -451,8 +451,6 @@ def tile_knnxlmultiheadsattention_pb_kernel(tc, q, qkv, kv_external, gate, Wo, b
             keep_clock(psum_scores, "scores")
         flip_queries(0)
         copy_queries(0)
-        exponentiate_gates()
-        prepare_gates()
         for half in range(2):
             regroup_values(0, half)
         for g in range(KEY_PASSES):
@@ -473,25 +471,31 @@ def tile_knnxlmultiheadsattention_pb_kernel(tc, q, qkv, kv_external, gate, Wo, b
                 fuse(done)
             if is_unit(code):
                 quantise_exponentials(code)
-            if is_unit(r):
-                quantise_values(r // 2, r % 2)
-                regroup_values(r // 2 + 1, r % 2)
             if queries_rest == 0 and 0 < queries < B * H // PAIR:
                 flip_queries(queries)
                 copy_queries(queries)
+            for t in range(Q_TILES):
+                for n in range(E // N_OUT):
+                    if r - 6 - n - t == H * Q_TILES - Q_TILES + t:
+                        project(0, t, n)
             if is_unit(new) and new > 0:
                 for g in range(KEY_PASSES):
                     scores(new, g)
+            if r == 1:
+                prepare_gates()
             if is_unit(flat):
                 row_divisor(flat)
                 if flat % Q_TILES == Q_TILES - 1:
                     row_weights(flat // Q_TILES)
-            if 0 <= wo_step < WO_PIECES and wo_rest == 1:
-                quantise_wo(wo_step)
             if merged_half(r - 5):
                 quantise_merged(*merged_half(r - 5))
             if is_unit(new) and new > 0:
                 row_shift(new)
+            if 0 <= wo_step < WO_PIECES and wo_rest == 1:
+                quantise_wo(wo_step)
+            if is_unit(r):
+                quantise_values(r // 2, r % 2)
+                regroup_values(r // 2 + 1, r % 2)
             if is_unit(r) and is_unit(new):
                 exponential(r)
             if is_unit(flat):
@@ -511,6 +515,8 @@ def tile_knnxlmultiheadsattention_pb_kernel(tc, q, qkv, kv_external, gate, Wo, b
             if not is_unit(new):
                 for g in range(KEY_PASSES):
                     exponential(r, g, 1)
+            if r == 0:
+                exponentiate_gates()
             if keys:
                 copy_keys(*keys, nc.scalar.copy if is_unit(r) else nc.vector.tensor_copy)
             if 0 <= wo_step < WO_PIECES and wo_rest == 0:
@@ -519,10 +525,6 @@ def tile_knnxlmultiheadsattention_pb_kernel(tc, q, qkv, kv_external, gate, Wo, b
             if merged_half(r - 4):
                 flip_merged(*merged_half(r - 4))
                 copy_merged(*merged_half(r - 4))
-            for t in range(Q_TILES):
-                for n in range(E // N_OUT):
-                    if r - 6 - n - t == H * Q_TILES - Q_TILES + t:
-                        project(0, t, n)
 
         before, last = UNITS - 2, UNITS - 1
         fuse(before - 1)

@@ -34,7 +34,6 @@ UNITS = B * H * Q_TILES
 HEAD_STEPS = 2
 KEY_LEAD = 3
 QUERY_LEAD = 2
-TAIL_W = 1
 WARM_UP = 2
 WO_PIECES = 8
 WO_START = 4
@@ -420,23 +419,36 @@ def tile_knnxlmultiheadsattention_pb_kernel(tc, q, qkv, kv_external, gate, Wo, b
             nc.vector.quantize_mx(out=m_codes[:].bitcast(FP8X4), scales=m_scales[:], in_=merged_words[(b, t, c)][:])
             merged_codes[(b, t, c)] = (m_codes, m_scales)
 
-        def project(b, t, n):
+        projections = {}
+
+        def multiply_merged(b, t, n, c, pool=psum_flip, tag="flip"):
+            if c == 0:
+                projected = pool.tile([P, N_OUT], F32, tag=tag)
+                projections[(b, t, n)] = projected
             cols = slice(n * N_OUT, (n + 1) * N_OUT)
-            projected = psum_flip.tile([P, N_OUT], F32, tag="flip")
-            for c in range(HD_PASSES):
-                m_codes, m_scales = merged_codes[(b, t, c)]
-                nc.tensor.matmul_mx(
-                    out=projected[:],
-                    lhsT=m_codes[:].bitcast(FP8X4),
-                    lhsT_scale=m_scales[:],
-                    rhs=wo_codes[:, c, cols].bitcast(FP8X4),
-                    rhs_scale=wo_scales[:, c, cols],
-                    start=(c == 0),
-                    stop=(c == HD_PASSES - 1),
-                )
+            m_codes, m_scales = merged_codes[(b, t, c)]
+            nc.tensor.matmul_mx(
+                out=projections[(b, t, n)][:],
+                lhsT=m_codes[:].bitcast(FP8X4),
+                lhsT_scale=m_scales[:],
+                rhs=wo_codes[:, c, cols].bitcast(FP8X4),
+                rhs_scale=wo_scales[:, c, cols],
+                start=(c == 0),
+                stop=(c == HD_PASSES - 1),
+            )
+
+        def store(b, t, n):
+            cols = slice(n * N_OUT, (n + 1) * N_OUT)
             result = results.tile([P, N_OUT], F32)
-            nc.vector.tensor_tensor(out=result[:], in0=projected[:], in1=bias_rows[:, cols], op=ALU.add)
+            nc.vector.tensor_tensor(
+                out=result[:], in0=projections[(b, t, n)][:], in1=bias_rows[:, cols], op=ALU.add
+            )
             nc.sync.dma_start(out=out[b, t * P : (t + 1) * P, cols], in_=result[:])
+
+        def project(b, t, n):
+            for c in range(HD_PASSES):
+                multiply_merged(b, t, n, c)
+            store(b, t, n)
 
         def is_unit(w):
             return 0 <= w < UNITS
@@ -501,12 +513,12 @@ def tile_knnxlmultiheadsattention_pb_kernel(tc, q, qkv, kv_external, gate, Wo, b
             if is_unit(flat):
                 for first in range(0, KEY_PASSES, PASSES_IN_BANK):
                     flip_exponentials(flat, first, PASSES_IN_BANK)
-            if keys:
-                flip_keys(*keys)
             if is_unit(r):
                 keep_clock(psum_mx, "sums")
             if is_unit(code):
                 multiply(code, psum_mx, "sums")
+            if keys:
+                flip_keys(*keys)
             if is_unit(r) and r % Q_TILES == Q_TILES - 1:
                 weigh_local(r // Q_TILES)
             if is_unit(flat):
@@ -527,17 +539,21 @@ def tile_knnxlmultiheadsattention_pb_kernel(tc, q, qkv, kv_external, gate, Wo, b
                 copy_merged(*merged_half(r - 4))
 
         before, last = UNITS - 2, UNITS - 1
+        tiles = [merged_half(before)[:2], merged_half(last)[:2]]
         fuse(before - 1)
         quantise_exponentials(before)
-        for g in range(2):
+        for g in range(KEY_PASSES):
             flip_exponentials(last, g, 1)
             group_exponentials(last, g, 1)
         multiply(before, psum_scores, "scores")
-        for g in range(2, KEY_PASSES):
-            flip_exponentials(last, g, 1)
-            group_exponentials(last, g, 1)
         row_weights(last // Q_TILES, 0)
-        fuse(before)
+        for g in range(KEY_PASSES):
+            quantise_exponentials(last, g, 1)
+            multiply(last, psum_scores, "scores", g, 1)
+            if g == 1:
+                fuse(before)
+                for n in range(E // N_OUT):
+                    multiply_merged(*tiles[1], n, 0, psum_scores, "scores")
         sum_parts = columns.tile([P, KEY_PASSES], F32)
         nc.vector.tensor_scalar(
             out=sum_parts[:],
@@ -549,19 +565,14 @@ def tile_knnxlmultiheadsattention_pb_kernel(tc, q, qkv, kv_external, gate, Wo, b
             accum_out=divisors[last // Q_TILES][:, Q_TILES - 1 :],
         )
         row_weights(last // Q_TILES, 1)
-        flip_merged(*merged_half(before))
-        copy_merged(*merged_half(before))
-        for n in range(TAIL_W):
-            keep_clock(psum_scores, "scores")
-        for g in range(KEY_PASSES):
-            quantise_exponentials(last, g, 1)
-            multiply(last, psum_scores, "scores", g, 1)
-        quantise_merged(*merged_half(before))
         fuse(last)
+        for tile in tiles:
+            flip_merged(*tile, 1)
+            copy_merged(*tile, 1)
+            quantise_merged(*tile, 1)
         for n in range(E // N_OUT):
-            project(*merged_half(before)[:2], n)
-        flip_merged(*merged_half(last))
-        copy_merged(*merged_half(last))
-        quantise_merged(*merged_half(last))
+            project(*tiles[0], n)
         for n in range(E // N_OUT):
-            project(*merged_half(last)[:2], n)
+            multiply_merged(*tiles[1], n, 1)
+        for n in range(E // N_OUT):
+            store(*tiles[1], n)

from contextlib import ExitStack

import concourse.masks as masks
import concourse.mybir as mybir

BF16 = mybir.dt.bfloat16
F32 = mybir.dt.float32
U32 = mybir.dt.uint32
U8 = mybir.dt.uint8
FP8X4 = mybir.dt.float8_e4m3fn_x4
ACT = mybir.ActivationFunctionType
ALU = mybir.AluOpType
AXIS = mybir.AxisListType

B, H, S, D, TOPK, E = 2, 8, 256, 128, 8, 1024
HD = H * D
J = S * TOPK
P = 128
PACK = 4
K_PASS = P * PACK
KEY_PASSES = J // K_PASS
HD_PASSES = HD // K_PASS
Q_TILES = S // P
BANK_BLOCKS = 8
K_WORDS = K_PASS // 2
PAIRS = 2
BANK_WORD_BLOCKS = 4
PASSES_IN_BANK = BANK_WORD_BLOCKS // PAIRS
N_OUT = 512
PAIR = 2
PAIR_BLOCKS = PAIR * Q_TILES
SCALE = D**-0.5
UNITS = B * H * Q_TILES
HEAD_STEPS = 2
KEY_LEAD = 3
QUERY_LEAD = 2
WARM_UP = 2
WO_PIECES = 8
WO_START = 4

FLOPS = 2 * (2 * B * H * S * J * D) + 2 * B * S * HD * E


def tile_knnxlmultiheadsattention_pb_kernel(tc, q, qkv, kv_external, gate, Wo, bo, out):
    nc = tc.nc

    memories = kv_external.rearrange("b s t c e -> b (s t) c e").rearrange(
        "b (g p x) c e -> b g p x c e", g=KEY_PASSES, p=P
    )
    key_rows = kv_external.rearrange("b s t c e -> b (s t) c e").rearrange("b (m i u) c e -> b m i u c e", i=P, u=PAIRS)
    q_rows = q.rearrange("b h (t p) d -> b p (h t) d", p=P)
    qkv_rows = qkv.rearrange("b h (t p) d -> b p (h t) d", p=P)

    with ExitStack() as ctx:
        ctx.enter_context(tc.manual_schedule())
        keep = ctx.enter_context(tc.tile_pool(name="keep", bufs=1))
        raw = ctx.enter_context(tc.tile_pool(name="raw", bufs=3))
        per_head = ctx.enter_context(tc.tile_pool(name="per_head", bufs=2))
        per_unit = ctx.enter_context(tc.tile_pool(name="per_unit", bufs=2))
        columns = ctx.enter_context(tc.tile_pool(name="columns", bufs=4))
        results = ctx.enter_context(tc.tile_pool(name="results", bufs=4))
        merged_code_pool = ctx.enter_context(tc.tile_pool(name="merged_codes", bufs=4))
        psum_scores = ctx.enter_context(tc.psum_pool(name="psum_scores", bufs=KEY_PASSES))
        psum_flip = ctx.enter_context(tc.psum_pool(name="psum_flip", bufs=3))
        psum_mx = ctx.enter_context(tc.psum_pool(name="psum_mx", bufs=1))

        ident = keep.tile([P, P], BF16)
        masks.make_identity(nc, ident[:])
        ident_words = keep.tile([P, P], F32)
        masks.make_identity(nc, ident_words[:])

        def flip(blocks):
            bank = psum_flip.tile([P, BANK_BLOCKS, P], BF16, tag="flip")
            for n, block in enumerate(blocks):
                nc.tensor.transpose(bank[:, n, :], block, ident[:])
            return bank

        def flip_words(blocks):
            bank = psum_flip.tile([P, BANK_WORD_BLOCKS, P], F32, tag="flip")
            for n, block in enumerate(blocks):
                nc.tensor.transpose(bank[:, n, :], block, ident_words[:])
            return bank

        def keep_clock(pool, tag):
            unread = pool.tile([P, P], F32, tag=tag)
            nc.tensor.matmul(out=unread[:], lhsT=ident_words[:], rhs=ident_words[:], start=True, stop=True)

        def unit_of(w):
            return w // (H * Q_TILES), (w % (H * Q_TILES)) // Q_TILES, w % Q_TILES

        gate_rows = keep.tile([P, H], BF16)
        ones = keep.tile([P, P], BF16)
        nc.vector.memset(gate_rows[:], 0.0)
        nc.vector.memset(ones[:], 1.0)
        q_raw = keep.tile([P, B, H * Q_TILES, D], BF16)
        qkv_raw = keep.tile([P, B, H * Q_TILES, D], BF16)
        wo_raw = keep.tile([P, E // P, HD], BF16)
        bias_rows = keep.tile([P, E], BF16)

        pair_tiles = {}

        def load_pair(n):
            b, first = n // (H // PAIR), (n % (H // PAIR)) * PAIR
            cols = slice(first * D, (first + PAIR) * D)
            blocks = slice(first * Q_TILES, (first + PAIR) * Q_TILES)
            k_raw = raw.tile([P, KEY_PASSES * 2, PAIRS, PAIR * D], BF16)
            v_raw = raw.tile([P, KEY_PASSES, PACK, PAIR * D], BF16)
            nc.sync.dma_start(out=q_raw[:, b, blocks], in_=q_rows[b][:, blocks])
            for m in range(KEY_PASSES * 2):
                nc.sync.dma_start(out=k_raw[:, m], in_=key_rows[b, m, :, :, 0, cols])
            for g in range(KEY_PASSES):
                nc.sync.dma_start(out=v_raw[:, g], in_=memories[b, g, :, :, 1, cols])
            nc.sync.dma_start(out=qkv_raw[:, b, blocks], in_=qkv_rows[b][:, blocks])
            pair_tiles[n] = (k_raw, v_raw)

        load_pair(0)
        nc.sync.dma_start(out=gate_rows[:1, :], in_=gate.rearrange("h a b -> (a b) h"))
        load_pair(1)
        nc.sync.dma_start(out=wo_raw[:], in_=Wo.rearrange("(a p) k -> p a k", p=P))
        load_pair(2)
        nc.sync.dma_start(out=bias_rows[:], in_=bo.partition_broadcast(P))

        g_local = keep.tile([P, H], F32)
        retrieved_divisor = keep.tile([P, H], F32)

        exp_minus = keep.tile([P, H], F32)
        exp_plus = keep.tile([P, H], F32)

        def exponentiate_gates():
            gates = psum_mx.tile([P, H], F32, tag="sums")
            nc.tensor.matmul(out=gates[:], lhsT=ones[:], rhs=gate_rows[:], start=True, stop=True)
            nc.scalar.activation(out=exp_minus[:], in_=gates[:], func=ACT.Exp, scale=-1.0)
            nc.scalar.activation(out=exp_plus[:], in_=gates[:], func=ACT.Exp)

        def prepare_gates():
            local_divisor = keep.tile([P, H], F32)
            nc.vector.tensor_scalar_add(out=local_divisor[:], in0=exp_minus[:], scalar1=1.0)
            nc.vector.tensor_scalar_add(out=retrieved_divisor[:], in0=exp_plus[:], scalar1=1.0)
            nc.vector.reciprocal(out=g_local[:], in_=local_divisor[:])

        q_t = keep.tile([P, B, H * Q_TILES, P], BF16)
        local_part = keep.tile([P, B, H * Q_TILES, D], F32)
        merged = [
            [keep.tile([P, HD], BF16, name="merged_%d_%d" % (b, t)) for t in range(Q_TILES)] for b in range(B)
        ]
        wo_codes = keep.tile([P, HD_PASSES, E], U32, align_bytes=64)
        wo_scales = keep.tile([P, HD_PASSES, E], U8, align_bytes=64)

        key_tiles = {}
        value_tiles = {}

        query_banks = {}

        def query_blocks(n):
            b, first = n // (H // PAIR), (n % (H // PAIR)) * PAIR_BLOCKS
            return b, slice(first, first + PAIR_BLOCKS)

        def flip_queries(n):
            b, blocks = query_blocks(n)
            query_banks[n] = flip([q_raw[:, b, m, :] for m in range(blocks.start, blocks.stop)])

        def copy_queries(n):
            b, blocks = query_blocks(n)
            nc.vector.tensor_copy(out=q_t[:, b, blocks, :], in_=query_banks[n][:, :PAIR_BLOCKS, :])

        key_banks = {}

        def flip_keys(number, passes):
            h = number % H
            k_raw = pair_tiles[number // PAIR][0]
            cols = slice((h % PAIR) * D, (h % PAIR + 1) * D)
            key_banks[number] = flip([k_raw[:, 2 * g + n, u, cols] for g in passes for u in range(PAIRS) for n in range(2)])

        def copy_keys(number, passes, copy):
            if passes[0] == 0:
                k_t = per_head.tile([P, KEY_PASSES * PACK, P], BF16)
                key_tiles[number] = k_t
            blocks = len(passes) * PACK
            first = passes[0] * PACK
            copy(out=key_tiles[number][:, first : first + blocks, :], in_=key_banks[number][:, :blocks, :])

        def key_step(step):
            number, part = step // HEAD_STEPS, step % HEAD_STEPS
            return (number, range(part * 2, part * 2 + 2)) if number < B * H else None

        grouped_values = {}

        def regroup_values(number, half):
            if number == B * H:
                return
            h = number % H
            v_raw = pair_tiles[number // PAIR][1]
            cols = slice((h % PAIR) * D, (h % PAIR + 1) * D)
            v_grouped = keep.tile([P, 2, D, PACK], BF16, align_bytes=64, name="v_grouped_%d" % half)
            for n in range(2):
                nc.gpsimd.tensor_scalar(
                    out=v_grouped[:, n].rearrange("p d (u j) -> p d u j", u=PAIRS),
                    in0=v_raw[:, half * 2 + n, :, cols].rearrange("p (j u) d -> p d u j", u=PAIRS),
                    scalar1=1.0,
                    scalar2=0.0,
                    op0=ALU.mult,
                    op1=ALU.add,
                )
            grouped_values[half] = v_grouped
            if h % PAIR == PAIR - 1 and half == 1 and number // PAIR + 3 < B * H // PAIR:
                load_pair(number // PAIR + 3)

        def quantise_values(number, half):
            if half == 0:
                v_codes = per_head.tile([P, KEY_PASSES * D], U32, align_bytes=64)
                v_scales = per_head.tile([P, KEY_PASSES * D], U8, align_bytes=64)
                value_tiles[number] = (v_codes, v_scales)
            v_codes, v_scales = value_tiles[number]
            cols = slice(half * 2 * D, (half * 2 + 2) * D)
            nc.vector.quantize_mx(
                out=v_codes[:, cols].bitcast(FP8X4),
                scales=v_scales[:, cols],
                in_=grouped_values[half][:].rearrange("p g d x -> p (g d x)"),
            )

        def weigh_local(number):
            b, h = number // H, number % H
            blocks = slice(h * Q_TILES, (h + 1) * Q_TILES)
            nc.gpsimd.tensor_scalar(
                out=local_part[:, b, blocks, :],
                in0=qkv_raw[:, b, blocks, :],
                scalar1=g_local[:, h : h + 1],
                scalar2=0.0,
                op0=ALU.mult,
                op1=ALU.add,
            )

        wo_banks = {}
        wo_pieces = {}

        def flip_wo(n):
            c, first = n // PACK, (n % PACK) * 2
            words = wo_raw[:].bitcast(F32)
            wo_banks[n] = flip_words(
                [words[:, first + a, c * K_WORDS + u : (c + 1) * K_WORDS : PAIRS] for a in range(2) for u in range(PAIRS)]
            )

        def copy_wo(n):
            wo_grouped = per_unit.tile([P, 2 * P * PACK], BF16, align_bytes=64)
            nc.scalar.copy(
                out=wo_grouped[:].bitcast(F32).rearrange("p (a e u) -> p a e u", a=2, u=PAIRS),
                in_=wo_banks[n][:].rearrange("p (a u) e -> p a e u", u=PAIRS),
            )
            wo_pieces[n] = wo_grouped

        def quantise_wo(n):
            c, first = n // PACK, (n % PACK) * 2 * P
            nc.vector.quantize_mx(
                out=wo_codes[:, c, first : first + 2 * P].bitcast(FP8X4),
                scales=wo_scales[:, c, first : first + 2 * P],
                in_=wo_pieces[n][:],
            )

        negated_scores = {}
        bank_minima = {}
        shifts = {}
        exponentials = {}
        row_sums = {}
        divisors = {}
        weights = {}
        flipped = {}
        grouped = {}
        coded = {}
        sums = {}

        def scores(w, g):
            b, h, t = unit_of(w)
            k_t = key_tiles[b * H + h]
            if g == 0:
                negated = per_unit.tile([P, J], F32)
                bank_min = columns.tile([P, KEY_PASSES], F32)
                negated_scores[w] = negated
                bank_minima[w] = bank_min
            s_bank = psum_scores.tile([P, K_PASS], F32, tag="scores")
            nc.tensor.matmul(
                out=s_bank[:],
                lhsT=q_t[:, b, h * Q_TILES + t, :],
                rhs=k_t[:, g * PACK : (g + 1) * PACK, :].rearrange("d x p -> d (x p)"),
                start=True,
                stop=True,
            )
            nc.vector.tensor_scalar(
                out=negated_scores[w][:, g * K_PASS : (g + 1) * K_PASS],
                in0=s_bank[:],
                scalar1=-SCALE,
                scalar2=None,
                op0=ALU.mult,
                op1=ALU.min,
                accum_out=bank_minima[w][:, g : g + 1],
            )

        def row_shift(w):
            shift = columns.tile([P, 1], F32)
            nc.vector.tensor_reduce(out=shift[:], in_=bank_minima[w][:], axis=AXIS.X, op=ALU.min)
            shifts[w] = shift

        def exponential(w, first=0, count=KEY_PASSES):
            if first == 0:
                e = per_unit.tile([P, J], BF16)
                row_sum = columns.tile([P, KEY_PASSES], F32)
                exponentials[w] = e
                row_sums[w] = row_sum
            cols = slice(first * K_PASS, (first + count) * K_PASS)
            nc.scalar.activation(
                out=exponentials[w][:, cols],
                in_=negated_scores[w][:, cols],
                func=ACT.Exp,
                bias=shifts[w][:],
                scale=-1.0,
                accum_out=row_sums[w][:, first : first + 1],
            )

        def row_divisor(w):
            b, h, t = unit_of(w)
            if t == 0:
                divisor = columns.tile([P, Q_TILES], F32)
                divisors[b * H + h] = divisor
            nc.gpsimd.tensor_scalar(
                out=divisors[b * H + h][:, t : t + 1],
                in0=row_sums[w][:, :1],
                scalar1=retrieved_divisor[:, h : h + 1],
                scalar2=0.0,
                op0=ALU.mult,
                op1=ALU.add,
            )

        def row_weights(number, t=None):
            if number not in weights:
                weight = columns.tile([P, Q_TILES], F32)
                weights[number] = weight
            cols = slice(0, Q_TILES) if t is None else slice(t, t + 1)
            nc.vector.reciprocal(out=weights[number][:, cols], in_=divisors[number][:, cols])

        def flip_exponentials(w, first, count):
            words = exponentials[w][:].bitcast(F32)
            flipped[(w, first)] = flip_words(
                [words[:, n * P : (n + 1) * P] for n in range(first * PAIRS, (first + count) * PAIRS)]
            )

        def group_exponentials(w, first, count):
            if first == 0:
                e_grouped = per_unit.tile([P, KEY_PASSES * P * PACK], BF16, align_bytes=64)
                grouped[w] = e_grouped
            words = grouped[w][:].bitcast(F32).rearrange("p (g r u) -> p g r u", g=KEY_PASSES, u=PAIRS)
            nc.scalar.copy(
                out=words[:, first : first + count],
                in_=flipped[(w, first)][:, : count * PAIRS, :].rearrange("p (g u) r -> p g r u", u=PAIRS),
            )

        def quantise_exponentials(w, first=0, count=KEY_PASSES):
            if first == 0:
                e_codes = per_unit.tile([P, KEY_PASSES * P], U32, align_bytes=64)
                e_scales = per_unit.tile([P, KEY_PASSES * P], U8, align_bytes=64)
                coded[w] = (e_codes, e_scales)
            e_codes, e_scales = coded[w]
            cols = slice(first * P, (first + count) * P)
            nc.vector.quantize_mx(
                out=e_codes[:, cols].bitcast(FP8X4),
                scales=e_scales[:, cols],
                in_=grouped[w][:, first * P * PACK : (first + count) * P * PACK],
            )

        def multiply(w, pool, tag, first=0, count=KEY_PASSES):
            b, h, t = unit_of(w)
            e_codes, e_scales = coded[w]
            v_codes, v_scales = value_tiles[b * H + h]
            if first == 0:
                retrieved = pool.tile([P, D], F32, tag=tag)
                sums[w] = retrieved
            for g in range(first, first + count):
                nc.tensor.matmul_mx(
                    out=sums[w][:],
                    lhsT=e_codes[:, g * P : (g + 1) * P].bitcast(FP8X4),
                    lhsT_scale=e_scales[:, g * P : (g + 1) * P],
                    rhs=v_codes[:, g * D : (g + 1) * D].bitcast(FP8X4),
                    rhs_scale=v_scales[:, g * D : (g + 1) * D],
                    start=(g == 0),
                    stop=(g == KEY_PASSES - 1),
                )

        def fuse(w):
            b, h, t = unit_of(w)
            nc.vector.scalar_tensor_tensor(
                out=merged[b][t][:, h * D : (h + 1) * D],
                in0=sums[w][:],
                scalar=weights[b * H + h][:, t : t + 1],
                in1=local_part[:, b, h * Q_TILES + t, :],
                op0=ALU.mult,
                op1=ALU.add,
            )

        merged_banks = {}
        merged_codes = {}

        def flip_merged(b, t, c):
            words = merged[b][t][:].bitcast(F32)
            merged_banks[(b, t, c)] = flip_words(
                [words[:, c * K_WORDS + u : (c + 1) * K_WORDS : PAIRS] for u in range(PAIRS)]
            )

        merged_words = {}

        def copy_merged(b, t, c):
            m_grouped = per_unit.tile([P, P * PACK], BF16, align_bytes=64)
            nc.scalar.copy(
                out=m_grouped[:].bitcast(F32).rearrange("p (r u) -> p r u", u=PAIRS),
                in_=merged_banks[(b, t, c)][:, :PAIRS, :].rearrange("p u r -> p r u"),
            )
            merged_words[(b, t, c)] = m_grouped

        def quantise_merged(b, t, c):
            m_codes = merged_code_pool.tile([P, P], U32, align_bytes=64)
            m_scales = merged_code_pool.tile([P, P], U8, align_bytes=64)
            nc.vector.quantize_mx(out=m_codes[:].bitcast(FP8X4), scales=m_scales[:], in_=merged_words[(b, t, c)][:])
            merged_codes[(b, t, c)] = (m_codes, m_scales)

        projections = {}

        def multiply_merged(b, t, n, c, pool=psum_flip, tag="flip"):
            if c == 0:
                projected = pool.tile([P, N_OUT], F32, tag=tag)
                projections[(b, t, n)] = projected
            cols = slice(n * N_OUT, (n + 1) * N_OUT)
            m_codes, m_scales = merged_codes[(b, t, c)]
            nc.tensor.matmul_mx(
                out=projections[(b, t, n)][:],
                lhsT=m_codes[:].bitcast(FP8X4),
                lhsT_scale=m_scales[:],
                rhs=wo_codes[:, c, cols].bitcast(FP8X4),
                rhs_scale=wo_scales[:, c, cols],
                start=(c == 0),
                stop=(c == HD_PASSES - 1),
            )

        def store(b, t, n):
            cols = slice(n * N_OUT, (n + 1) * N_OUT)
            result = results.tile([P, N_OUT], F32)
            nc.vector.tensor_tensor(
                out=result[:], in0=projections[(b, t, n)][:], in1=bias_rows[:, cols], op=ALU.add
            )
            nc.sync.dma_start(out=out[b, t * P : (t + 1) * P, cols], in_=result[:])

        def project(b, t, n):
            for c in range(HD_PASSES):
                multiply_merged(b, t, n, c)
            store(b, t, n)

        def is_unit(w):
            return 0 <= w < UNITS

        def merged_half(w):
            if not is_unit(w):
                return None
            b, h, t = unit_of(w)
            return (b, t, h // PACK) if h % PACK == PACK - 1 else None

        for n in range(WARM_UP):
            keep_clock(psum_scores, "scores")
        flip_queries(0)
        copy_queries(0)
        for half in range(2):
            regroup_values(0, half)
        for g in range(KEY_PASSES):
            flip_keys(0, [g])
            copy_keys(0, [g], nc.vector.tensor_copy if g % 2 == 0 else nc.scalar.copy)
            if g > 0:
                scores(0, g - 1)
            else:
                keep_clock(psum_mx, "sums")
        scores(0, KEY_PASSES - 1)
        row_shift(0)
        for r in range(-1, UNITS):
            new, flat, code, done = r + 1, r - 1, r - 2, r - 3
            keys = key_step(r + KEY_LEAD)
            wo_step, wo_rest = divmod(r - WO_START, 2)
            queries, queries_rest = divmod(r + QUERY_LEAD, PAIR_BLOCKS)
            if is_unit(done):
                fuse(done)
            if is_unit(code):
                quantise_exponentials(code)
            if queries_rest == 0 and 0 < queries < B * H // PAIR:
                flip_queries(queries)
                copy_queries(queries)
            for t in range(Q_TILES):
                for n in range(E // N_OUT):
                    if r - 6 - n - t == H * Q_TILES - Q_TILES + t:
                        project(0, t, n)
            if is_unit(new) and new > 0:
                for g in range(KEY_PASSES):
                    scores(new, g)
            if r == 1:
                prepare_gates()
            if is_unit(flat):
                row_divisor(flat)
                if flat % Q_TILES == Q_TILES - 1:
                    row_weights(flat // Q_TILES)
            if merged_half(r - 5):
                quantise_merged(*merged_half(r - 5))
            if is_unit(new) and new > 0:
                row_shift(new)
            if 0 <= wo_step < WO_PIECES and wo_rest == 1:
                quantise_wo(wo_step)
            if is_unit(r):
                quantise_values(r // 2, r % 2)
                regroup_values(r // 2 + 1, r % 2)
            if is_unit(r) and is_unit(new):
                exponential(r)
            if is_unit(flat):
                for first in range(0, KEY_PASSES, PASSES_IN_BANK):
                    flip_exponentials(flat, first, PASSES_IN_BANK)
            if is_unit(r):
                keep_clock(psum_mx, "sums")
            if is_unit(code):
                multiply(code, psum_mx, "sums")
            if keys:
                flip_keys(*keys)
            if is_unit(r) and r % Q_TILES == Q_TILES - 1:
                weigh_local(r // Q_TILES)
            if is_unit(flat):
                for first in range(0, KEY_PASSES, PASSES_IN_BANK):
                    group_exponentials(flat, first, PASSES_IN_BANK)
            if not is_unit(new):
                for g in range(KEY_PASSES):
                    exponential(r, g, 1)
            if r == 0:
                exponentiate_gates()
            if keys:
                copy_keys(*keys, nc.scalar.copy if is_unit(r) else nc.vector.tensor_copy)
            if 0 <= wo_step < WO_PIECES and wo_rest == 0:
                flip_wo(wo_step)
                copy_wo(wo_step)
            if merged_half(r - 4):
                flip_merged(*merged_half(r - 4))
                copy_merged(*merged_half(r - 4))

        before, last = UNITS - 2, UNITS - 1
        tiles = [merged_half(before)[:2], merged_half(last)[:2]]
        fuse(before - 1)
        quantise_exponentials(before)
        for g in range(KEY_PASSES):
            flip_exponentials(last, g, 1)
            group_exponentials(last, g, 1)
        multiply(before, psum_scores, "scores")
        row_weights(last // Q_TILES, 0)
        for g in range(KEY_PASSES):
            quantise_exponentials(last, g, 1)
            multiply(last, psum_scores, "scores", g, 1)
            if g == 1:
                fuse(before)
                for n in range(E // N_OUT):
                    multiply_merged(*tiles[1], n, 0, psum_scores, "scores")
        sum_parts = columns.tile([P, KEY_PASSES], F32)
        nc.vector.tensor_scalar(
            out=sum_parts[:],
            in0=row_sums[last][:],
            scalar1=retrieved_divisor[:, H - 1 :],
            scalar2=None,
            op0=ALU.mult,
            op1=ALU.add,
            accum_out=divisors[last // Q_TILES][:, Q_TILES - 1 :],
        )
        row_weights(last // Q_TILES, 1)
        fuse(last)
        for tile in tiles:
            flip_merged(*tile, 1)
            copy_merged(*tile, 1)
            quantise_merged(*tile, 1)
        for n in range(E // N_OUT):
            project(*tiles[0], n)
        for n in range(E // N_OUT):
            multiply_merged(*tiles[1], n, 1)
        for n in range(E // N_OUT):
            store(*tiles[1], n)
